import numpy as np
import ml_dtypes


def mxq(x, axis, fmt="e4m3"):
    dtype, down = {"e4m3": (ml_dtypes.float8_e4m3fn, 7), "e5m2": (ml_dtypes.float8_e5m2, 14)}[fmt]
    v = np.moveaxis(np.asarray(x, np.float32).astype(ml_dtypes.bfloat16).astype(np.float64), axis, -1)
    blocks = v.reshape(v.shape[:-1] + (-1, 32))
    amax = np.abs(blocks).max(-1, keepdims=True)
    byte = np.maximum(np.where(amax > 0, np.frexp(amax)[1] - 1 + 127, 0) - down, 1)
    scale = np.exp2(byte - 127.0)
    codes = (blocks / scale).astype(np.float32).astype(dtype).astype(np.float64)
    return np.moveaxis((codes * scale).reshape(v.shape), -1, axis)


WIDE = False


def mx_kscale(k):
    if not WIDE:
        return np.ones(k)
    levels = np.array([10, -10, 5, -5, 0])
    if k % 512:
        return np.exp2(np.random.permutation(np.resize(levels, k // 32))).repeat(32)
    a = np.empty((k // 512, 16))
    for p in range(k // 512):
        a[p, :8] = np.random.permutation(np.resize(levels, 8))
        for g in range(8):
            far = levels[np.abs(levels - a[p, g]) >= 10]
            a[p, g + 8] = far[np.random.randint(len(far))]
    return np.exp2(a.ravel()).repeat(32)


BF16 = ml_dtypes.bfloat16


def bf(x):
    return np.asarray(x, np.float32).astype(BF16)


def f64(x):
    return np.asarray(x).astype(np.float64)


N, DB, DV, DL, DC, T, DO = 2048, 500, 1012, 256, 128, 12, 256
KB, KV = DB + T, DV + T
LN_EPS = 1e-5
ERF_TERMS = 100


def erf(v):
    a = np.clip(v, -6.0, 6.0)
    term = a.copy()
    tot = a.copy()
    for n in range(1, ERF_TERMS):
        term = term * (2.0 * a * a) / (2.0 * n + 1.0)
        tot = tot + term
    return 2.0 / np.sqrt(np.pi) * np.exp(-a * a) * tot


def gelu_erf(v):
    return 0.5 * v * (1.0 + erf(v / np.sqrt(2.0)))


def t2v(t, w0, w, b):
    v0 = w0 * t + b[0]
    v = np.sin(w * t[:, None] + b[1:])
    return np.concatenate([v0[:, None], v], axis=-1)


def branch(z, gamma, beta, W):
    mu = z.mean(-1, keepdims=True)
    var = np.square(z - mu).mean(-1, keepdims=True)
    zn = (z - mu) / np.sqrt(var + LN_EPS) * gamma + beta
    return gelu_erf(mxq(zn, 1, "e4m3") @ mxq(W, 0, "e4m3"))


def rows(d):
    return np.random.standard_normal((N, d)) * (0.5 + np.random.uniform(size=(N, 1))) + 0.3 * np.random.standard_normal((N, 1))


def setup_inputs():
    sb, sv = mx_kscale(KB), mx_kscale(KV)
    return {"x_bill": bf(rows(DB)), "ts_bill": bf(np.random.uniform(size=N)),
            "x_bill_version": bf(rows(DV)), "ts_bill_version": bf(np.random.uniform(size=N)),
            "w0": bf(3.0 + 0.5 * np.random.standard_normal(1)),
            "w": bf(3.0 * np.random.standard_normal(T - 1)),
            "b": bf(1.5 + 0.5 * np.random.standard_normal(T)),
            "gamma_bill": bf((1.0 + 0.1 * np.random.standard_normal(KB)) * sb),
            "beta_bill": bf(0.1 * np.random.standard_normal(KB) * sb),
            "W_bill": bf(np.random.standard_normal((KB, DO)) * np.sqrt(2.0 / KB) / sb[:, None]),
            "gamma_bill_version": bf((1.0 + 0.1 * np.random.standard_normal(KV)) * sv),
            "beta_bill_version": bf(0.1 * np.random.standard_normal(KV) * sv),
            "W_bill_version": bf(np.random.standard_normal((KV, DO)) * np.sqrt(2.0 / KV) / sv[:, None])}


def reference(x_bill, ts_bill, x_bill_version, ts_bill_version, w0, w, b,
              gamma_bill, beta_bill, W_bill, gamma_bill_version, beta_bill_version, W_bill_version):
    w0, w, b = f64(w0), f64(w), f64(b)
    zb = np.concatenate([f64(x_bill), t2v(f64(ts_bill), w0, w, b)], axis=1)
    zv = np.concatenate([f64(x_bill_version), t2v(f64(ts_bill_version), w0, w, b)], axis=1)
    out_bill = branch(zb, f64(gamma_bill), f64(beta_bill), f64(W_bill))
    out_bv = branch(zv, f64(gamma_bill_version), f64(beta_bill_version), f64(W_bill_version))
    return np.stack([out_bill, out_bv], axis=0)

@@ -1,0 +1,356 @@
+from contextlib import ExitStack
+import math
+
+import concourse.mybir as mybir
+from concourse.masks import make_identity
+
+F32 = mybir.dt.float32
+BF16 = mybir.dt.bfloat16
+U32 = mybir.dt.uint32
+U8 = mybir.dt.uint8
+FP8X4 = mybir.dt.float8_e4m3fn_x4
+ACT = mybir.ActivationFunctionType
+ALU = mybir.AluOpType
+
+P = 128
+PACK = 4
+K_PASS = P * PACK
+ROWS = 2048
+ROW_TILES = ROWS // P
+GROUP = 4
+GROUPS = ROW_TILES // GROUP
+GROUP_COLS = GROUP * P
+T2V = 12
+LAST = 32
+LAST_P = LAST // PACK
+D_OUT = 256
+LN_EPS = 1e-5
+BN_MAX = 512
+BN_DIM = 6
+KINDS = 2
+
+ROUND_MAGIC = 12582912.0
+TWO_PI_HIGH = 6.28125
+TWO_PI_LOW = 2.0 * math.pi - TWO_PI_HIGH
+SIN_LIMIT = 3.1415925
+
+SCALAR_NORM_TILES = 2
+
+FLOPS = 2 * ROWS * D_OUT * (512 + 1024)
+
+
+def tile_featureprojector_pa_kernel(
+    tc,
+    x_bill,
+    ts_bill,
+    x_bill_version,
+    ts_bill_version,
+    w0,
+    w,
+    b,
+    gamma_bill,
+    beta_bill,
+    W_bill,
+    gamma_bill_version,
+    beta_bill_version,
+    W_bill_version,
+    out,
+):
+    nc = tc.nc
+    kinds = [
+        {"x": x_bill, "ts": ts_bill, "gamma": gamma_bill, "beta": beta_bill, "W": W_bill, "first": 0},
+        {
+            "x": x_bill_version,
+            "ts": ts_bill_version,
+            "gamma": gamma_bill_version,
+            "beta": beta_bill_version,
+            "W": W_bill_version,
+            "first": 4,
+        },
+    ]
+    for kind in kinds:
+        kind["d"] = kind["x"].shape[1]
+        kind["k"] = kind["d"] + T2V
+        kind["tiles"] = kind["k"] // P
+        kind["passes"] = kind["k"] // K_PASS
+        kind["chunks"] = (kind["d"] + BN_MAX - 1) // BN_MAX
+    all_tiles = sum(kind["tiles"] for kind in kinds)
+    all_passes = sum(kind["passes"] for kind in kinds)
+
+    with ExitStack() as stack:
+        const = stack.enter_context(tc.tile_pool(name="const", bufs=1))
+        x_pool = stack.enter_context(tc.tile_pool(name="x", bufs=1))
+        small = stack.enter_context(tc.tile_pool(name="small", bufs=4))
+        xn_pool = stack.enter_context(tc.tile_pool(name="xn", bufs=2))
+        work = stack.enter_context(tc.tile_pool(name="work", bufs=4))
+        turned_pool = stack.enter_context(tc.psum_pool(name="turned", bufs=6))
+        acc_pool = stack.enter_context(tc.psum_pool(name="acc", bufs=2))
+
+        ts_sb = const.tile([P, KINDS, ROW_TILES], BF16)
+        for j, kind in enumerate(kinds):
+            nc.sync.dma_start(out=ts_sb[:, j, :], in_=kind["ts"].rearrange("(p i) -> p i", i=ROW_TILES))
+        w0_sb = const.tile([P, 1], BF16)
+        nc.sync.dma_start(out=w0_sb[:], in_=w0.partition_broadcast(P))
+        w_sb = const.tile([P, T2V - 1], BF16)
+        nc.sync.dma_start(out=w_sb[:], in_=w.partition_broadcast(P))
+        b_sb = const.tile([P, T2V], BF16)
+        nc.sync.dma_start(out=b_sb[:], in_=b.partition_broadcast(P))
+
+        groups = [(j, g) for j in range(KINDS) for g in range(GROUPS)]
+        x_sb = {}
+
+        def load_rows(j, g):
+            x_tile = x_pool.tile([P, GROUP, kinds[j]["d"]], BF16, name="x_%d_%d" % (j, g))
+            rows = kinds[j]["x"].rearrange("(p i) d -> p i d", i=ROW_TILES)
+            nc.sync.dma_start(out=x_tile[:], in_=rows[:, g * GROUP : (g + 1) * GROUP, :])
+            x_sb[(j, g)] = x_tile
+
+        load_rows(*groups[0])
+
+        gb_rows = const.tile([P, K_PASS], BF16)
+        nc.vector.memset(gb_rows[:], 0.0)
+        w_raw = const.tile([P, all_tiles, D_OUT], BF16)
+        for kind in kinds:
+            first, passes = kind["first"] // PACK, kind["passes"]
+            nc.sync.dma_start(
+                out=gb_rows[first : first + passes, :], in_=kind["gamma"].rearrange("(c k) -> c k", k=K_PASS)
+            )
+            nc.sync.dma_start(
+                out=gb_rows[all_passes + first : all_passes + first + passes, :],
+                in_=kind["beta"].rearrange("(c k) -> c k", k=K_PASS),
+            )
+        for kind in kinds:
+            for c in range(kind["passes"]):
+                first = kind["first"] + c * PACK
+                nc.sync.dma_start(
+                    out=w_raw[:, first : first + PACK, :],
+                    in_=kind["W"][c * K_PASS : (c + 1) * K_PASS, :].rearrange("(p t) n -> p t n", t=PACK),
+                )
+
+        for j, g in groups[1:]:
+            load_rows(j, g)
+
+        identity = const.tile([P, P], F32)
+        make_identity(nc, identity[:])
+
+        n_ts = KINDS * ROW_TILES
+        n_sin = T2V - 1
+        ts_flat = ts_sb[:].rearrange("p j i -> p (j i)")
+        linear = const.tile([P, n_ts], F32)
+        nc.vector.tensor_scalar(
+            out=linear[:], in0=ts_flat, scalar1=w0_sb[:, 0:1], scalar2=b_sb[:, 0:1], op0=ALU.mult, op1=ALU.add
+        )
+        phase = const.tile([P, n_ts, n_sin], F32)
+        nc.vector.tensor_tensor(
+            out=phase[:],
+            in0=ts_flat.unsqueeze(2).to_broadcast([P, n_ts, n_sin]),
+            in1=w_sb[:].unsqueeze(1).to_broadcast([P, n_ts, n_sin]),
+            op=ALU.mult,
+        )
+        nc.vector.tensor_tensor(
+            out=phase[:], in0=phase[:], in1=b_sb[:, 1:T2V].unsqueeze(1).to_broadcast([P, n_ts, n_sin]), op=ALU.add
+        )
+        phase_flat = phase[:].rearrange("p n s -> p (n s)")
+        turns = const.tile([P, n_ts * n_sin], F32)
+        nc.vector.tensor_scalar(
+            out=turns[:], in0=phase_flat, scalar1=1.0 / (2.0 * math.pi), scalar2=ROUND_MAGIC, op0=ALU.mult, op1=ALU.add
+        )
+        nc.vector.tensor_scalar(out=turns[:], in0=turns[:], scalar1=ROUND_MAGIC, scalar2=None, op0=ALU.subtract)
+        reduced = const.tile([P, n_ts, n_sin], F32)
+        reduced_flat = reduced[:].rearrange("p n s -> p (n s)")
+        nc.vector.scalar_tensor_tensor(
+            out=reduced_flat, in0=turns[:], scalar=-TWO_PI_HIGH, in1=phase_flat, op0=ALU.mult, op1=ALU.add
+        )
+        nc.vector.scalar_tensor_tensor(
+            out=reduced_flat, in0=turns[:], scalar=-TWO_PI_LOW, in1=reduced_flat, op0=ALU.mult, op1=ALU.add
+        )
+        nc.vector.tensor_scalar(
+            out=reduced_flat, in0=reduced_flat, scalar1=-SIN_LIMIT, scalar2=SIN_LIMIT, op0=ALU.max, op1=ALU.min
+        )
+        last = const.tile([P, n_ts, LAST], F32)
+        t2v = last[:, :, LAST - T2V : LAST]
+        nc.scalar.activation(out=last[:, :, LAST - T2V + 1 : LAST], in_=reduced[:], func=ACT.Sin)
+        nc.scalar.copy(out=last[:, :, LAST - T2V : LAST - T2V + 1], in_=linear[:].unsqueeze(2))
+
+        neg_half = const.tile([P, GROUP], F32)
+        nc.vector.memset(neg_half[:], -0.5)
+
+        gamma_beta = const.tile([P, PACK, 2 * all_passes], F32)
+        w_codes = const.tile([P, all_passes, D_OUT], U32, align_bytes=64)
+        w_scales = const.tile([P, all_passes, D_OUT], U8, align_bytes=64)
+
+        def turn_gamma_beta():
+            gb_rows_f32 = const.tile([P, PACK, P], F32)
+            nc.vector.tensor_copy(out=gb_rows_f32[:], in_=gb_rows[:].rearrange("c (p t) -> c t p", t=PACK))
+            gb_turned = turned_pool.tile([P, PACK, P], F32, tag="turned")
+            for t in range(PACK):
+                nc.tensor.transpose(gb_turned[:, t, :], gb_rows_f32[:, t, :], identity[:])
+            nc.vector.tensor_copy(out=gamma_beta[:], in_=gb_turned[:, :, 0 : 2 * all_passes])
+
+        def quantise_w():
+            w_grouped = const.tile([P, all_passes, D_OUT, PACK], BF16, align_bytes=64)
+            for c in range(all_passes):
+                nc.scalar.copy(
+                    out=w_grouped[:, c, :, :], in_=w_raw[:, c * PACK : (c + 1) * PACK, :].rearrange("p t n -> p n t")
+                )
+            for c in range(all_passes):
+                nc.vector.quantize_mx(
+                    out=w_codes[:, c, :].bitcast(FP8X4),
+                    scales=w_scales[:, c, :],
+                    in_=w_grouped[:, c, :, :].rearrange("p n t -> p (n t)"),
+                )
+
+        row_scale = {}
+        row_shift = {}
+        normalised = {}
+        planes = {}
+        zn_codes = {}
+        zn_scales = {}
+        sums = {}
+
+        def statistics(j, g):
+            kind = kinds[j]
+            chunks = kind["chunks"]
+            width = kind["d"] // chunks
+            stats = small.tile([P, GROUP, chunks + 1, BN_DIM], F32, tag="stats")
+            mean_var = small.tile([P, GROUP, 2], F32, tag="mean_var")
+            for i in range(GROUP):
+                for h in range(chunks):
+                    nc.vector.bn_stats(out=stats[:, i, h, :], in_=x_sb[(j, g)][:, i, h * width : (h + 1) * width])
+            for i in range(GROUP):
+                nc.vector.bn_stats(out=stats[:, i, chunks, :], in_=t2v[:, j * ROW_TILES + g * GROUP + i, :])
+            rows = slice(j * ROW_TILES + g * GROUP, j * ROW_TILES + (g + 1) * GROUP)
+            nc.scalar.copy(
+                out=last[:, rows, 0 : LAST - T2V], in_=x_sb[(j, g)][:, :, kind["d"] - (LAST - T2V) : kind["d"]]
+            )
+            for i in range(GROUP):
+                nc.vector.bn_aggr(out=mean_var[:, i, :], in_=stats[:, i, :, :].rearrange("p h s -> p (h s)"))
+            var_eps = small.tile([P, GROUP], F32, tag="var_eps")
+            nc.gpsimd.tensor_scalar(
+                out=var_eps[:], in0=mean_var[:, :, 1], scalar1=LN_EPS, scalar2=1.0, op0=ALU.add, op1=ALU.mult
+            )
+            scale = small.tile([P, GROUP], F32, tag="scale")
+            nc.gpsimd.tensor_tensor(out=scale[:], in0=var_eps[:], in1=neg_half[:], op=ALU.pow)
+            mean_scaled = small.tile([P, GROUP], F32, tag="mean_scaled")
+            nc.gpsimd.tensor_tensor(out=mean_scaled[:], in0=mean_var[:, :, 0], in1=scale[:], op=ALU.mult)
+            shift = small.tile([P, GROUP], F32, tag="shift")
+            nc.gpsimd.tensor_scalar(
+                out=shift[:], in0=mean_scaled[:], scalar1=-1.0, scalar2=0.0, op0=ALU.mult, op1=ALU.add
+            )
+            row_scale[(j, g)] = scale
+            row_shift[(j, g)] = shift
+
+        def normalise(j, g):
+            kind = kinds[j]
+            passes = kind["passes"]
+            scale, shift = row_scale[(j, g)], row_shift[(j, g)]
+            xn = xn_pool.tile([P, GROUP, passes, PACK, P], F32, tag="xn")
+            for i in range(GROUP):
+                parts = []
+                for c in range(passes):
+                    width = P if c < passes - 1 else P - LAST_P
+                    src = x_sb[(j, g)][:, i, c * K_PASS : c * K_PASS + width * PACK]
+                    parts.append((xn[:, i, c, :, 0:width], src))
+                parts.append((xn[:, i, passes - 1, :, P - LAST_P : P], last[:, j * ROW_TILES + g * GROUP + i, :]))
+                for dst, src in [(dst, src.rearrange("r (p t) -> r t p", t=PACK)) for dst, src in parts]:
+                    if i < SCALAR_NORM_TILES:
+                        nc.scalar.activation(
+                            out=dst, in_=src, func=ACT.Identity, scale=scale[:, i : i + 1], bias=shift[:, i : i + 1]
+                        )
+                    else:
+                        nc.vector.tensor_scalar(
+                            out=dst,
+                            in0=src,
+                            scalar1=scale[:, i : i + 1],
+                            scalar2=shift[:, i : i + 1],
+                            op0=ALU.mult,
+                            op1=ALU.add,
+                        )
+            normalised[(j, g)] = xn
+
+        def turn(j, g):
+            kind = kinds[j]
+            xn = normalised[(j, g)]
+            for c in range(kind["passes"]):
+                zn_planes = work.tile([P, PACK, GROUP_COLS], BF16, tag="zn_planes")
+                for t in range(PACK):
+                    turned = turned_pool.tile([P, GROUP_COLS], F32, tag="turned")
+                    for i in range(GROUP):
+                        nc.tensor.transpose(
+                            turned[:, i * P : (i + 1) * P],
+                            xn[:, i, c, t, :],
+                            identity[:],
+                        )
+                    col = kind["first"] // PACK + c
+                    nc.scalar.activation(
+                        out=zn_planes[:, t, :],
+                        in_=turned[:],
+                        func=ACT.Identity,
+                        scale=gamma_beta[:, t, col : col + 1],
+                        bias=gamma_beta[:, t, all_passes + col : all_passes + col + 1],
+                    )
+                planes[(j, g, c)] = zn_planes
+
+        def quantise(j, g):
+            passes = kinds[j]["passes"]
+            grouped = {}
+            for c in range(passes):
+                grouped[c] = work.tile([P, GROUP_COLS, PACK], BF16, tag="grouped", align_bytes=64, name="grouped")
+                nc.vector.tensor_copy(
+                    out=grouped[c][:].rearrange("p (n r) t -> p n t r", r=4),
+                    in_=planes[(j, g, c)][:].rearrange("p t (n r) -> p n t r", r=4),
+                )
+            for c in range(passes):
+                zn_codes[(j, g, c)] = work.tile([P, GROUP_COLS], U32, tag="codes", align_bytes=64, name="codes")
+                zn_scales[(j, g, c)] = work.tile([P, GROUP_COLS], U8, tag="scales", align_bytes=64, name="scales")
+                nc.vector.quantize_mx(
+                    out=zn_codes[(j, g, c)][:].bitcast(FP8X4),
+                    scales=zn_scales[(j, g, c)][:],
+                    in_=grouped[c][:].rearrange("p n t -> p (n t)"),
+                )
+
+        def multiply(j, g):
+            passes = kinds[j]["passes"]
+            first_pass = kinds[j]["first"] // PACK
+            for half in range(GROUP // 2):
+                acc = acc_pool.tile([P, 2, D_OUT], F32, tag="acc")
+                for s in range(2):
+                    i = half * 2 + s
+                    for c in range(passes):
+                        nc.tensor.matmul_mx(
+                            out=acc[:, s, :],
+                            lhsT=zn_codes[(j, g, c)][:, i * P : (i + 1) * P].bitcast(FP8X4),
+                            lhsT_scale=zn_scales[(j, g, c)][:, i * P : (i + 1) * P],
+                            rhs=w_codes[:, first_pass + c, :].bitcast(FP8X4),
+                            rhs_scale=w_scales[:, first_pass + c, :],
+                            start=(c == 0),
+                            stop=(c == passes - 1),
+                        )
+                sums[(j, g, half)] = acc
+
+        def gelu_and_store(j, g):
+            result = work.tile([P, GROUP, D_OUT], F32, tag="result")
+            for half in range(GROUP // 2):
+                nc.scalar.activation(out=result[:, half * 2 : half * 2 + 2, :], in_=sums[(j, g, half)][:], func=ACT.Gelu)
+            out_rows = out[j].rearrange("(p i) n -> p i n", i=ROW_TILES)
+            nc.sync.dma_start(out=out_rows[:, g * GROUP : (g + 1) * GROUP, :], in_=result[:])
+
+        n = len(groups)
+        with tc.manual_schedule():
+            statistics(*groups[0])
+            turn_gamma_beta()
+            statistics(*groups[1])
+            quantise_w()
+            for a in range(n + 2):
+                if a < n:
+                    normalise(*groups[a])
+                if a >= 2:
+                    gelu_and_store(*groups[a - 2])
+                if 1 <= a <= n:
+                    quantise(*groups[a - 1])
+                if a < n:
+                    turn(*groups[a])
+                if 1 <= a <= n:
+                    multiply(*groups[a - 1])
+                if a + 2 < n:
+                    statistics(*groups[a + 2])

@@ -21,20 +21,26 @@ GROUP = 4
 GROUPS = ROW_TILES // GROUP
 GROUP_COLS = GROUP * P
 T2V = 12
+N_SIN = T2V - 1
 LAST = 32
+LAST_X = LAST - T2V
 LAST_P = LAST // PACK
 D_OUT = 256
 LN_EPS = 1e-5
 BN_MAX = 512
-BN_DIM = 6
-KINDS = 2
+TRIPLE = 3
+BILL, VERSION = 0, 1
 
 ROUND_MAGIC = 12582912.0
 TWO_PI_HIGH = 6.28125
 TWO_PI_LOW = 2.0 * math.pi - TWO_PI_HIGH
 SIN_LIMIT = 3.1415925
 
-SCALAR_NORM_TILES = 2
+VECTOR_NORM_TILES = 1
+VECTOR_NORM_TILES_LATE = 1
+VECTOR_PLANES_LATE = 1
+LATE = 3
+LOOKAHEAD = 4
 
 FLOPS = 2 * ROWS * D_OUT * (512 + 1024)
 
@@ -65,38 +71,35 @@ def tile_featureprojector_pa_kernel(
             "gamma": gamma_bill_version,
             "beta": beta_bill_version,
             "W": W_bill_version,
-            "first": 4,
+            "first": 1,
         },
     ]
     for kind in kinds:
         kind["d"] = kind["x"].shape[1]
-        kind["k"] = kind["d"] + T2V
-        kind["tiles"] = kind["k"] // P
-        kind["passes"] = kind["k"] // K_PASS
+        kind["passes"] = (kind["d"] + T2V) // K_PASS
         kind["chunks"] = (kind["d"] + BN_MAX - 1) // BN_MAX
-    all_tiles = sum(kind["tiles"] for kind in kinds)
     all_passes = sum(kind["passes"] for kind in kinds)
+
+    groups = [(BILL, 0), (BILL, 1)] + [(VERSION, g) for g in range(GROUPS)] + [(BILL, 2), (BILL, 3)]
+    units = [(j, g, c) for j, g in groups for c in range(kinds[j]["passes"])]
 
     with ExitStack() as stack:
         const = stack.enter_context(tc.tile_pool(name="const", bufs=1))
         x_pool = stack.enter_context(tc.tile_pool(name="x", bufs=1))
         small = stack.enter_context(tc.tile_pool(name="small", bufs=4))
-        xn_pool = stack.enter_context(tc.tile_pool(name="xn", bufs=2))
+        xn_pool = stack.enter_context(tc.tile_pool(name="xn", bufs=3))
         work = stack.enter_context(tc.tile_pool(name="work", bufs=4))
         turned_pool = stack.enter_context(tc.psum_pool(name="turned", bufs=6))
         acc_pool = stack.enter_context(tc.psum_pool(name="acc", bufs=2))
 
-        ts_sb = const.tile([P, KINDS, ROW_TILES], BF16)
+        ts_sb = const.tile([P, len(kinds), ROW_TILES], BF16)
         for j, kind in enumerate(kinds):
             nc.sync.dma_start(out=ts_sb[:, j, :], in_=kind["ts"].rearrange("(p i) -> p i", i=ROW_TILES))
-        w0_sb = const.tile([P, 1], BF16)
-        nc.sync.dma_start(out=w0_sb[:], in_=w0.partition_broadcast(P))
-        w_sb = const.tile([P, T2V - 1], BF16)
+        w_sb = const.tile([P, N_SIN], BF16)
         nc.sync.dma_start(out=w_sb[:], in_=w.partition_broadcast(P))
         b_sb = const.tile([P, T2V], BF16)
         nc.sync.dma_start(out=b_sb[:], in_=b.partition_broadcast(P))
 
-        groups = [(j, g) for j in range(KINDS) for g in range(GROUPS)]
         x_sb = {}
 
         def load_rows(j, g):
@@ -105,252 +108,424 @@ def tile_featureprojector_pa_kernel(
             nc.sync.dma_start(out=x_tile[:], in_=rows[:, g * GROUP : (g + 1) * GROUP, :])
             x_sb[(j, g)] = x_tile
 
-        load_rows(*groups[0])
-
         gb_rows = const.tile([P, K_PASS], BF16)
-        nc.vector.memset(gb_rows[:], 0.0)
-        w_raw = const.tile([P, all_tiles, D_OUT], BF16)
-        for kind in kinds:
-            first, passes = kind["first"] // PACK, kind["passes"]
-            nc.sync.dma_start(
-                out=gb_rows[first : first + passes, :], in_=kind["gamma"].rearrange("(c k) -> c k", k=K_PASS)
-            )
-            nc.sync.dma_start(
-                out=gb_rows[all_passes + first : all_passes + first + passes, :],
-                in_=kind["beta"].rearrange("(c k) -> c k", k=K_PASS),
-            )
-        for kind in kinds:
-            for c in range(kind["passes"]):
-                first = kind["first"] + c * PACK
-                nc.sync.dma_start(
-                    out=w_raw[:, first : first + PACK, :],
-                    in_=kind["W"][c * K_PASS : (c + 1) * K_PASS, :].rearrange("(p t) n -> p t n", t=PACK),
-                )
+        nc.gpsimd.memset(gb_rows[:], 0.0)
+        w_raw = const.tile([P, all_passes, PACK, D_OUT], BF16)
 
-        for j, g in groups[1:]:
+        def load_gamma_beta(kind):
+            first, passes = kind["first"], kind["passes"]
+            for row, name in ((first, "gamma"), (all_passes + first, "beta")):
+                nc.sync.dma_start(out=gb_rows[row : row + passes, :], in_=kind[name].rearrange("(c k) -> c k", k=K_PASS))
+
+        def load_w(kind):
+            for c in range(kind["passes"]):
+                rows = kind["W"][c * K_PASS : (c + 1) * K_PASS, :]
+                nc.sync.dma_start(out=w_raw[:, kind["first"] + c, :, :], in_=rows.rearrange("(p t) n -> p t n", t=PACK))
+
+        load_rows(*groups[0])
+        w0_sb = const.tile([P, 1], BF16)
+        nc.sync.dma_start(out=w0_sb[:], in_=w0.partition_broadcast(P))
+        for kind in kinds:
+            load_gamma_beta(kind)
+        load_rows(*groups[1])
+        load_w(kinds[BILL])
+        load_rows(*groups[2])
+        load_w(kinds[VERSION])
+        for j, g in groups[3:]:
             load_rows(j, g)
 
         identity = const.tile([P, P], F32)
         make_identity(nc, identity[:])
-
-        n_ts = KINDS * ROW_TILES
-        n_sin = T2V - 1
-        ts_flat = ts_sb[:].rearrange("p j i -> p (j i)")
-        linear = const.tile([P, n_ts], F32)
-        nc.vector.tensor_scalar(
-            out=linear[:], in0=ts_flat, scalar1=w0_sb[:, 0:1], scalar2=b_sb[:, 0:1], op0=ALU.mult, op1=ALU.add
-        )
-        phase = const.tile([P, n_ts, n_sin], F32)
-        nc.vector.tensor_tensor(
-            out=phase[:],
-            in0=ts_flat.unsqueeze(2).to_broadcast([P, n_ts, n_sin]),
-            in1=w_sb[:].unsqueeze(1).to_broadcast([P, n_ts, n_sin]),
-            op=ALU.mult,
-        )
-        nc.vector.tensor_tensor(
-            out=phase[:], in0=phase[:], in1=b_sb[:, 1:T2V].unsqueeze(1).to_broadcast([P, n_ts, n_sin]), op=ALU.add
-        )
-        phase_flat = phase[:].rearrange("p n s -> p (n s)")
-        turns = const.tile([P, n_ts * n_sin], F32)
-        nc.vector.tensor_scalar(
-            out=turns[:], in0=phase_flat, scalar1=1.0 / (2.0 * math.pi), scalar2=ROUND_MAGIC, op0=ALU.mult, op1=ALU.add
-        )
-        nc.vector.tensor_scalar(out=turns[:], in0=turns[:], scalar1=ROUND_MAGIC, scalar2=None, op0=ALU.subtract)
-        reduced = const.tile([P, n_ts, n_sin], F32)
-        reduced_flat = reduced[:].rearrange("p n s -> p (n s)")
-        nc.vector.scalar_tensor_tensor(
-            out=reduced_flat, in0=turns[:], scalar=-TWO_PI_HIGH, in1=phase_flat, op0=ALU.mult, op1=ALU.add
-        )
-        nc.vector.scalar_tensor_tensor(
-            out=reduced_flat, in0=turns[:], scalar=-TWO_PI_LOW, in1=reduced_flat, op0=ALU.mult, op1=ALU.add
-        )
-        nc.vector.tensor_scalar(
-            out=reduced_flat, in0=reduced_flat, scalar1=-SIN_LIMIT, scalar2=SIN_LIMIT, op0=ALU.max, op1=ALU.min
-        )
-        last = const.tile([P, n_ts, LAST], F32)
-        t2v = last[:, :, LAST - T2V : LAST]
-        nc.scalar.activation(out=last[:, :, LAST - T2V + 1 : LAST], in_=reduced[:], func=ACT.Sin)
-        nc.scalar.copy(out=last[:, :, LAST - T2V : LAST - T2V + 1], in_=linear[:].unsqueeze(2))
-
         neg_half = const.tile([P, GROUP], F32)
-        nc.vector.memset(neg_half[:], -0.5)
+        nc.gpsimd.memset(neg_half[:], -0.5)
+
+        last = const.tile([P, len(kinds), ROW_TILES, LAST], F32)
+        w0_f32 = const.tile([P, 1], F32)
+        b0_f32 = const.tile([P, 1], F32)
+        reduced = const.tile([P, len(kinds), ROW_TILES, N_SIN], F32)
+
+        def phase_steps(j, engine):
+            shape = [P, ROW_TILES, N_SIN]
+            phase = const.tile(shape, F32, name="phase_%d" % j)
+            turns = const.tile(shape, F32, name="turns_%d" % j)
+            part = const.tile(shape, F32, name="part_%d" % j)
+            red = reduced[:, j, :, :]
+            by_vector = engine is nc.vector
+            ts_wide = ts_sb[:, j, :].unsqueeze(2).to_broadcast(shape)
+            w_wide = w_sb[:].unsqueeze(1).to_broadcast(shape)
+            b_wide = b_sb[:, 1:T2V].unsqueeze(1).to_broadcast(shape)
+
+            def tensor(dst, in0, in1, op):
+                return lambda: engine.tensor_tensor(out=dst, in0=in0, in1=in1, op=op)
+
+            def affine(dst, in0, factor, term):
+                return lambda: engine.tensor_scalar(
+                    out=dst, in0=in0, scalar1=factor, scalar2=term, op0=ALU.mult, op1=ALU.add
+                )
+
+            def take_off(dst, src, two_pi):
+                if by_vector:
+                    return [
+                        lambda: nc.vector.scalar_tensor_tensor(
+                            out=dst, in0=turns[:], scalar=-two_pi, in1=src, op0=ALU.mult, op1=ALU.add
+                        )
+                    ]
+                return [affine(part[:], turns[:], -two_pi, 0.0), tensor(dst, src, part[:], ALU.add)]
+
+            return [
+                tensor(phase[:], ts_wide, w_wide, ALU.mult),
+                tensor(phase[:], phase[:], b_wide, ALU.add),
+                affine(turns[:], phase[:], 1.0 / (2.0 * math.pi), ROUND_MAGIC),
+                affine(turns[:], turns[:], 1.0, -ROUND_MAGIC),
+                *take_off(red, phase[:], TWO_PI_HIGH),
+                *take_off(red, red, TWO_PI_LOW),
+            ]
+
+        def limit_phase(j):
+            red = reduced[:, j, :, :]
+            nc.vector.tensor_scalar(out=red, in0=red, scalar1=-SIN_LIMIT, scalar2=SIN_LIMIT, op0=ALU.max, op1=ALU.min)
+
+        def time_features(j):
+            nc.scalar.activation(out=last[:, j, :, LAST_X + 1 : LAST], in_=reduced[:, j, :, :], func=ACT.Sin)
+            nc.scalar.activation(
+                out=last[:, j, :, LAST_X : LAST_X + 1],
+                in_=ts_sb[:, j, :].unsqueeze(2),
+                func=ACT.Identity,
+                scale=w0_f32[:],
+                bias=b0_f32[:],
+            )
 
         gamma_beta = const.tile([P, PACK, 2 * all_passes], F32)
         w_codes = const.tile([P, all_passes, D_OUT], U32, align_bytes=64)
         w_scales = const.tile([P, all_passes, D_OUT], U8, align_bytes=64)
+        w_grouped = const.tile([P, all_passes, D_OUT, PACK], BF16, align_bytes=64)
 
         def turn_gamma_beta():
             gb_rows_f32 = const.tile([P, PACK, P], F32)
-            nc.vector.tensor_copy(out=gb_rows_f32[:], in_=gb_rows[:].rearrange("c (p t) -> c t p", t=PACK))
+            nc.gpsimd.tensor_scalar(
+                out=gb_rows_f32[:],
+                in0=gb_rows[:].rearrange("c (p t) -> c t p", t=PACK),
+                scalar1=1.0,
+                scalar2=0.0,
+                op0=ALU.mult,
+                op1=ALU.add,
+            )
             gb_turned = turned_pool.tile([P, PACK, P], F32, tag="turned")
             for t in range(PACK):
                 nc.tensor.transpose(gb_turned[:, t, :], gb_rows_f32[:, t, :], identity[:])
-            nc.vector.tensor_copy(out=gamma_beta[:], in_=gb_turned[:, :, 0 : 2 * all_passes])
+            nc.scalar.copy(out=gamma_beta[:], in_=gb_turned[:, :, 0 : 2 * all_passes])
 
-        def quantise_w():
-            w_grouped = const.tile([P, all_passes, D_OUT, PACK], BF16, align_bytes=64)
-            for c in range(all_passes):
-                nc.scalar.copy(
-                    out=w_grouped[:, c, :, :], in_=w_raw[:, c * PACK : (c + 1) * PACK, :].rearrange("p t n -> p n t")
-                )
-            for c in range(all_passes):
-                nc.vector.quantize_mx(
-                    out=w_codes[:, c, :].bitcast(FP8X4),
-                    scales=w_scales[:, c, :],
-                    in_=w_grouped[:, c, :, :].rearrange("p n t -> p (n t)"),
-                )
+        def interleave_w(c):
+            nc.gpsimd.tensor_scalar(
+                out=w_grouped[:, c, :, :],
+                in0=w_raw[:, c, :, :].rearrange("p t n -> p n t"),
+                scalar1=1.0,
+                scalar2=0.0,
+                op0=ALU.mult,
+                op1=ALU.add,
+            )
 
+        def quantise_w(c):
+            nc.vector.quantize_mx(
+                out=w_codes[:, c, :].bitcast(FP8X4),
+                scales=w_scales[:, c, :],
+                in_=w_grouped[:, c, :, :].rearrange("p n t -> p (n t)"),
+            )
+
+        scalar_rows = {groups[0]: [3], groups[1]: [1, 2, 3]}
+        count_x = const.tile([P, 1], F32)
+        nc.gpsimd.memset(count_x[:], float(kinds[BILL]["d"]))
+        stats = {}
+        mean_var = {}
         row_scale = {}
         row_shift = {}
         normalised = {}
+        banks = {}
         planes = {}
+        grouped = {}
         zn_codes = {}
         zn_scales = {}
         sums = {}
 
-        def statistics(j, g):
-            kind = kinds[j]
-            chunks = kind["chunks"]
-            width = kind["d"] // chunks
-            stats = small.tile([P, GROUP, chunks + 1, BN_DIM], F32, tag="stats")
-            mean_var = small.tile([P, GROUP, 2], F32, tag="mean_var")
-            for i in range(GROUP):
-                for h in range(chunks):
-                    nc.vector.bn_stats(out=stats[:, i, h, :], in_=x_sb[(j, g)][:, i, h * width : (h + 1) * width])
-            for i in range(GROUP):
-                nc.vector.bn_stats(out=stats[:, i, chunks, :], in_=t2v[:, j * ROW_TILES + g * GROUP + i, :])
-            rows = slice(j * ROW_TILES + g * GROUP, j * ROW_TILES + (g + 1) * GROUP)
-            nc.scalar.copy(
-                out=last[:, rows, 0 : LAST - T2V], in_=x_sb[(j, g)][:, :, kind["d"] - (LAST - T2V) : kind["d"]]
+        def end_of_x(j, g):
+            rows = slice(g * GROUP, (g + 1) * GROUP)
+            d = kinds[j]["d"]
+            nc.scalar.copy(out=last[:, j, rows, 0:LAST_X], in_=x_sb[(j, g)][:, :, d - LAST_X : d])
+
+        def new_stats(j, g):
+            n = 2 * (kinds[j]["chunks"] + 1)
+            stats[(j, g)] = small.tile([P, GROUP, n * TRIPLE], F32, tag="stats", name="stats")
+
+        def row_statistics(j, g, i):
+            chunks = kinds[j]["chunks"]
+            width = kinds[j]["d"] // chunks
+            for h in range(chunks):
+                nc.vector.bn_stats(
+                    out=stats[(j, g)][:, i, 2 * h * TRIPLE : 2 * (h + 1) * TRIPLE],
+                    in_=x_sb[(j, g)][:, i, h * width : (h + 1) * width],
+                )
+
+        def scalar_statistics(j, g, tiles):
+            d = kinds[j]["d"]
+            junk = small.tile([P, d], BF16, tag="junk", name="junk")
+            neg_mean = small.tile([P, GROUP], F32, tag="minus", name="minus")
+            st = stats[(j, g)]
+            for i in tiles:
+                nc.scalar.activation(
+                    out=junk[:],
+                    in_=x_sb[(j, g)][:, i, :],
+                    func=ACT.Copy,
+                    scale=1.0 / d,
+                    accum_out=st[:, i, TRIPLE + 1 : TRIPLE + 2],
+                )
+            for i in tiles:
+                nc.scalar.mul(neg_mean[:, i : i + 1], st[:, i, TRIPLE + 1 : TRIPLE + 2], -1.0)
+                nc.scalar.copy(out=st[:, i, TRIPLE : TRIPLE + 1], in_=count_x[:])
+            for i in tiles:
+                nc.scalar.activation(
+                    out=junk[:],
+                    in_=x_sb[(j, g)][:, i, :],
+                    func=ACT.Square,
+                    bias=neg_mean[:, i : i + 1],
+                    accum_out=st[:, i, TRIPLE + 2 : TRIPLE + 3],
+                )
+
+        def time_statistics(j, g, i):
+            n = 2 * kinds[j]["chunks"]
+            nc.vector.bn_stats(
+                out=stats[(j, g)][:, i, n * TRIPLE : (n + 2) * TRIPLE], in_=last[:, j, g * GROUP + i, LAST_X:LAST]
             )
+
+        def aggregate(j, g):
+            mean_var[(j, g)] = small.tile([P, GROUP, 2], F32, tag="mean_var", name="mean_var")
             for i in range(GROUP):
-                nc.vector.bn_aggr(out=mean_var[:, i, :], in_=stats[:, i, :, :].rearrange("p h s -> p (h s)"))
+                start = TRIPLE if i in scalar_rows.get((j, g), ()) else 0
+                nc.vector.bn_aggr(out=mean_var[(j, g)][:, i, :], in_=stats[(j, g)][:, i, start:])
+
+        def invert(j, g):
+            mv = mean_var[(j, g)]
             var_eps = small.tile([P, GROUP], F32, tag="var_eps")
-            nc.gpsimd.tensor_scalar(
-                out=var_eps[:], in0=mean_var[:, :, 1], scalar1=LN_EPS, scalar2=1.0, op0=ALU.add, op1=ALU.mult
-            )
+            nc.gpsimd.tensor_scalar(out=var_eps[:], in0=mv[:, :, 1], scalar1=1.0, scalar2=LN_EPS, op0=ALU.mult, op1=ALU.add)
             scale = small.tile([P, GROUP], F32, tag="scale")
             nc.gpsimd.tensor_tensor(out=scale[:], in0=var_eps[:], in1=neg_half[:], op=ALU.pow)
-            mean_scaled = small.tile([P, GROUP], F32, tag="mean_scaled")
-            nc.gpsimd.tensor_tensor(out=mean_scaled[:], in0=mean_var[:, :, 0], in1=scale[:], op=ALU.mult)
+            neg_mean = small.tile([P, GROUP], F32, tag="neg_mean")
+            nc.gpsimd.tensor_scalar(out=neg_mean[:], in0=mv[:, :, 0], scalar1=-1.0, scalar2=0.0, op0=ALU.mult, op1=ALU.add)
             shift = small.tile([P, GROUP], F32, tag="shift")
-            nc.gpsimd.tensor_scalar(
-                out=shift[:], in0=mean_scaled[:], scalar1=-1.0, scalar2=0.0, op0=ALU.mult, op1=ALU.add
-            )
+            nc.gpsimd.tensor_tensor(out=shift[:], in0=neg_mean[:], in1=scale[:], op=ALU.mult)
             row_scale[(j, g)] = scale
             row_shift[(j, g)] = shift
 
-        def normalise(j, g):
-            kind = kinds[j]
-            passes = kind["passes"]
+        def normalise(u, vector_tiles):
+            j, g, c = units[u]
             scale, shift = row_scale[(j, g)], row_shift[(j, g)]
-            xn = xn_pool.tile([P, GROUP, passes, PACK, P], F32, tag="xn")
+            xn = xn_pool.tile([P, GROUP, PACK, P], F32, tag="xn", name="xn")
+            is_last = c == kinds[j]["passes"] - 1
+            width = P - LAST_P if is_last else P
             for i in range(GROUP):
-                parts = []
-                for c in range(passes):
-                    width = P if c < passes - 1 else P - LAST_P
-                    src = x_sb[(j, g)][:, i, c * K_PASS : c * K_PASS + width * PACK]
-                    parts.append((xn[:, i, c, :, 0:width], src))
-                parts.append((xn[:, i, passes - 1, :, P - LAST_P : P], last[:, j * ROW_TILES + g * GROUP + i, :]))
-                for dst, src in [(dst, src.rearrange("r (p t) -> r t p", t=PACK)) for dst, src in parts]:
-                    if i < SCALAR_NORM_TILES:
-                        nc.scalar.activation(
-                            out=dst, in_=src, func=ACT.Identity, scale=scale[:, i : i + 1], bias=shift[:, i : i + 1]
-                        )
-                    else:
-                        nc.vector.tensor_scalar(
-                            out=dst,
-                            in0=src,
-                            scalar1=scale[:, i : i + 1],
-                            scalar2=shift[:, i : i + 1],
-                            op0=ALU.mult,
-                            op1=ALU.add,
-                        )
-            normalised[(j, g)] = xn
-
-        def turn(j, g):
-            kind = kinds[j]
-            xn = normalised[(j, g)]
-            for c in range(kind["passes"]):
-                zn_planes = work.tile([P, PACK, GROUP_COLS], BF16, tag="zn_planes")
-                for t in range(PACK):
-                    turned = turned_pool.tile([P, GROUP_COLS], F32, tag="turned")
-                    for i in range(GROUP):
-                        nc.tensor.transpose(
-                            turned[:, i * P : (i + 1) * P],
-                            xn[:, i, c, t, :],
-                            identity[:],
-                        )
-                    col = kind["first"] // PACK + c
+                dst = xn[:, i, :, 0:width]
+                src = x_sb[(j, g)][:, i, c * K_PASS : c * K_PASS + width * PACK].rearrange("r (p t) -> r t p", t=PACK)
+                if i < GROUP - vector_tiles:
                     nc.scalar.activation(
-                        out=zn_planes[:, t, :],
-                        in_=turned[:],
-                        func=ACT.Identity,
-                        scale=gamma_beta[:, t, col : col + 1],
-                        bias=gamma_beta[:, t, all_passes + col : all_passes + col + 1],
+                        out=dst, in_=src, func=ACT.Identity, scale=scale[:, i : i + 1], bias=shift[:, i : i + 1]
                     )
-                planes[(j, g, c)] = zn_planes
+                else:
+                    nc.vector.tensor_scalar(
+                        out=dst, in0=src, scalar1=scale[:, i : i + 1], scalar2=shift[:, i : i + 1], op0=ALU.mult, op1=ALU.add
+                    )
+            if is_last:
+                for i in range(GROUP):
+                    nc.gpsimd.tensor_scalar(
+                        out=xn[:, i, :, width:P],
+                        in0=last[:, j, g * GROUP + i, :].rearrange("r (p t) -> r t p", t=PACK),
+                        scalar1=scale[:, i : i + 1],
+                        scalar2=shift[:, i : i + 1],
+                        op0=ALU.mult,
+                        op1=ALU.add,
+                    )
+            normalised[u] = xn
 
-        def quantise(j, g):
-            passes = kinds[j]["passes"]
-            grouped = {}
-            for c in range(passes):
-                grouped[c] = work.tile([P, GROUP_COLS, PACK], BF16, tag="grouped", align_bytes=64, name="grouped")
-                nc.vector.tensor_copy(
-                    out=grouped[c][:].rearrange("p (n r) t -> p n t r", r=4),
-                    in_=planes[(j, g, c)][:].rearrange("p t (n r) -> p n t r", r=4),
-                )
-            for c in range(passes):
-                zn_codes[(j, g, c)] = work.tile([P, GROUP_COLS], U32, tag="codes", align_bytes=64, name="codes")
-                zn_scales[(j, g, c)] = work.tile([P, GROUP_COLS], U8, tag="scales", align_bytes=64, name="scales")
-                nc.vector.quantize_mx(
-                    out=zn_codes[(j, g, c)][:].bitcast(FP8X4),
-                    scales=zn_scales[(j, g, c)][:],
-                    in_=grouped[c][:].rearrange("p n t -> p (n t)"),
-                )
+        def turn(u):
+            for t in range(PACK):
+                bank = turned_pool.tile([P, GROUP_COLS], F32, tag="turned", name="turned")
+                for i in range(GROUP):
+                    nc.tensor.transpose(bank[:, i * P : (i + 1) * P], normalised[u][:, i, t, :], identity[:])
+                banks[(u, t)] = bank
 
-        def multiply(j, g):
-            passes = kinds[j]["passes"]
-            first_pass = kinds[j]["first"] // PACK
-            for half in range(GROUP // 2):
-                acc = acc_pool.tile([P, 2, D_OUT], F32, tag="acc")
+        def leave(u, vector_planes, cols):
+            j, g, c = units[u]
+            if u not in planes:
+                planes[u] = work.tile([P, PACK, GROUP_COLS], BF16, tag="planes", name="planes")
+            col = kinds[j]["first"] + c
+            for t in range(PACK):
+                scale = gamma_beta[:, t, col : col + 1]
+                bias = gamma_beta[:, t, all_passes + col : all_passes + col + 1]
+                dst, src = planes[u][:, t, cols], banks[(u, t)][:, cols]
+                if t < PACK - vector_planes:
+                    nc.scalar.activation(out=dst, in_=src, func=ACT.Identity, scale=scale, bias=bias)
+                else:
+                    nc.vector.tensor_scalar(out=dst, in0=src, scalar1=scale, scalar2=bias, op0=ALU.mult, op1=ALU.add)
+
+        def interleave(u, cols):
+            if u not in grouped:
+                grouped[u] = work.tile([P, GROUP_COLS, PACK], BF16, tag="grouped", align_bytes=64, name="grouped")
+            nc.vector.tensor_copy(
+                out=grouped[u][:, cols, :].rearrange("p (n r) t -> p n t r", r=4),
+                in_=planes[u][:, :, cols].rearrange("p t (n r) -> p n t r", r=4),
+            )
+
+        def quantise(u, cols):
+            if u not in zn_codes:
+                zn_codes[u] = work.tile([P, GROUP_COLS], U32, tag="codes", align_bytes=64, name="codes")
+                zn_scales[u] = work.tile([P, GROUP_COLS], U8, tag="scales", align_bytes=64, name="scales")
+            nc.vector.quantize_mx(
+                out=zn_codes[u][:, cols].bitcast(FP8X4),
+                scales=zn_scales[u][:, cols],
+                in_=grouped[u][:, cols, :].rearrange("p n t -> p (n t)"),
+            )
+
+        def multiply(u, halves):
+            j, g, c = units[u]
+            passes = c + 1
+            for half in halves:
+                acc = acc_pool.tile([P, 2, D_OUT], F32, tag="acc", name="acc")
                 for s in range(2):
                     i = half * 2 + s
-                    for c in range(passes):
+                    for k in range(passes):
+                        unit = u - c + k
                         nc.tensor.matmul_mx(
                             out=acc[:, s, :],
-                            lhsT=zn_codes[(j, g, c)][:, i * P : (i + 1) * P].bitcast(FP8X4),
-                            lhsT_scale=zn_scales[(j, g, c)][:, i * P : (i + 1) * P],
-                            rhs=w_codes[:, first_pass + c, :].bitcast(FP8X4),
-                            rhs_scale=w_scales[:, first_pass + c, :],
-                            start=(c == 0),
-                            stop=(c == passes - 1),
+                            lhsT=zn_codes[unit][:, i * P : (i + 1) * P].bitcast(FP8X4),
+                            lhsT_scale=zn_scales[unit][:, i * P : (i + 1) * P],
+                            rhs=w_codes[:, kinds[j]["first"] + k, :].bitcast(FP8X4),
+                            rhs_scale=w_scales[:, kinds[j]["first"] + k, :],
+                            start=(k == 0),
+                            stop=(k == passes - 1),
                         )
-                sums[(j, g, half)] = acc
+                sums[(u, half)] = acc
 
-        def gelu_and_store(j, g):
-            result = work.tile([P, GROUP, D_OUT], F32, tag="result")
-            for half in range(GROUP // 2):
-                nc.scalar.activation(out=result[:, half * 2 : half * 2 + 2, :], in_=sums[(j, g, half)][:], func=ACT.Gelu)
+        def gelu_and_store(u, halves):
+            j, g, c = units[u]
             out_rows = out[j].rearrange("(p i) n -> p i n", i=ROW_TILES)
-            nc.sync.dma_start(out=out_rows[:, g * GROUP : (g + 1) * GROUP, :], in_=result[:])
+            result = work.tile([P, GROUP, D_OUT], F32, tag="result", name="result")
+            for half in halves:
+                tiles = slice(half * 2, half * 2 + 2)
+                nc.scalar.activation(out=result[:, tiles, :], in_=sums[(u, half)][:], func=ACT.Gelu)
+            tiles = slice(halves[0] * 2, halves[-1] * 2 + 2)
+            first_row = g * GROUP
+            nc.sync.dma_start(
+                out=out_rows[:, first_row + tiles.start : first_row + tiles.stop, :], in_=result[:, tiles, :]
+            )
 
-        n = len(groups)
+        pieces = []
+        for j, g in groups:
+            n = kinds[j]["passes"]
+            for c in range(n):
+                pieces.append((j, g, range(c * GROUP // n, (c + 1) * GROUP // n), c == 0, c == n - 1))
+
+        whole = slice(0, GROUP_COLS)
+        both = [0, 1]
+        n_units = len(units)
+
+        def last_pass(u):
+            j, g, c = units[u]
+            return c == kinds[j]["passes"] - 1
+
+        def open_statistics(k):
+            j, g, tiles, is_first, is_last = pieces[k]
+            if is_first:
+                new_stats(j, g)
+                end_of_x(j, g)
+
+        def statistics_steps(k):
+            j, g, tiles, is_first, is_last = pieces[k]
+            steps = [lambda i=i: row_statistics(j, g, i) for i in tiles if i not in scalar_rows.get((j, g), ())]
+            steps.append(lambda: [time_statistics(j, g, i) for i in tiles])
+            return steps
+
+        def close_statistics(k):
+            j, g, tiles, is_first, is_last = pieces[k]
+            if is_last:
+                aggregate(j, g)
+                invert(j, g)
+
+        def run(steps):
+            for step in steps:
+                step()
+
+        def vector_norm(u):
+            return VECTOR_NORM_TILES if u < n_units - LATE else VECTOR_NORM_TILES_LATE
+
+        def vector_planes(u):
+            return 0 if u < n_units - LATE else VECTOR_PLANES_LATE
+
         with tc.manual_schedule():
-            statistics(*groups[0])
+            nc.scalar.copy(out=b0_f32[:], in_=b_sb[:, 0:1])
+            bill_phase = phase_steps(BILL, nc.vector)
+            version_phase = phase_steps(VERSION, nc.gpsimd)
+            open_statistics(0)
+            rows = statistics_steps(0)
+            new_stats(*groups[1])
+            rows_1 = statistics_steps(1)
+            run(bill_phase[:2])
+            for k in range(2, 5):
+                bill_phase[k]()
+                rows[k - 2]()
+            bill_phase[5]()
+            rows_1[0]()
+            limit_phase(BILL)
+            scalar_statistics(*groups[0], scalar_rows[groups[0]])
+            nc.scalar.copy(out=w0_f32[:], in_=w0_sb[:])
+            time_features(BILL)
             turn_gamma_beta()
-            statistics(*groups[1])
-            quantise_w()
-            for a in range(n + 2):
-                if a < n:
-                    normalise(*groups[a])
-                if a >= 2:
-                    gelu_and_store(*groups[a - 2])
-                if 1 <= a <= n:
-                    quantise(*groups[a - 1])
-                if a < n:
-                    turn(*groups[a])
-                if 1 <= a <= n:
-                    multiply(*groups[a - 1])
-                if a + 2 < n:
-                    statistics(*groups[a + 2])
+            run(version_phase[:3])
+            rows[-1]()
+            end_of_x(*groups[1])
+            scalar_statistics(*groups[1], scalar_rows[groups[1]][:1])
+            close_statistics(0)
+            open_statistics(2)
+            rows_1[-1]()
+            rows_2 = statistics_steps(2)
+            rows_2[0]()
+            normalise(0, 2)
+            scalar_statistics(*groups[1], scalar_rows[groups[1]][1:])
+            turn(0)
+            run(version_phase[3:])
+            limit_phase(VERSION)
+            close_statistics(1)
+            rows_2[1]()
+            time_features(VERSION)
+            rows_2[2]()
+            normalise(1, 1)
+            interleave_w(0)
+            run(statistics_steps(3))
+            for s in range(n_units + 2):
+                k = s + LOOKAHEAD
+                if k - 1 < n_units:
+                    close_statistics(k - 1)
+                if s in (0, 2):
+                    interleave_w(1 + s // 2)
+                if s < n_units:
+                    leave(s, vector_planes(s), whole)
+                for later in [k, k + 1] if s == 0 else [k + 1]:
+                    if later < n_units:
+                        open_statistics(later)
+                steps = statistics_steps(k) if k < n_units else []
+                run(steps[:-1])
+                if 0 <= s - 1 < n_units:
+                    interleave(s - 1, whole)
+                run(steps[-1:])
+                if 0 <= s - 2 and last_pass(s - 2):
+                    gelu_and_store(s - 2, both)
+                if s == 1:
+                    quantise_w(0)
+                if s == 3:
+                    for c in range(1, all_passes):
+                        quantise_w(c)
+                if 0 <= s - 1 < n_units:
+                    quantise(s - 1, whole)
+                if s + 2 < n_units:
+                    normalise(s + 2, vector_norm(s + 2))
+                if s + 1 < n_units:
+                    turn(s + 1)
+                if 0 <= s - 1 < n_units and last_pass(s - 1):
+                    multiply(s - 1, both)

@@ -36,8 +36,8 @@ TWO_PI_HIGH = 6.28125
 TWO_PI_LOW = 2.0 * math.pi - TWO_PI_HIGH
 SIN_LIMIT = 3.1415925
 
-VECTOR_NORM_TILES = 1
-VECTOR_NORM_TILES_LATE = 1
+VECTOR_NORM_TILES = 2
+VECTOR_NORM_TILES_LATE = 2
 VECTOR_PLANES_LATE = 1
 LATE = 3
 LOOKAHEAD = 4
@@ -216,14 +216,7 @@ def tile_featureprojector_pa_kernel(
             nc.scalar.copy(out=gamma_beta[:], in_=gb_turned[:, :, 0 : 2 * all_passes])
 
         def interleave_w(c):
-            nc.gpsimd.tensor_scalar(
-                out=w_grouped[:, c, :, :],
-                in0=w_raw[:, c, :, :].rearrange("p t n -> p n t"),
-                scalar1=1.0,
-                scalar2=0.0,
-                op0=ALU.mult,
-                op1=ALU.add,
-            )
+            nc.scalar.copy(out=w_grouped[:, c, :, :], in_=w_raw[:, c, :, :].rearrange("p t n -> p n t"))
 
         def quantise_w(c):
             nc.vector.quantize_mx(
@@ -232,7 +225,7 @@ def tile_featureprojector_pa_kernel(
                 in_=w_grouped[:, c, :, :].rearrange("p n t -> p (n t)"),
             )
 
-        scalar_rows = {groups[0]: [3], groups[1]: [1, 2, 3]}
+        scalar_rows = {}
         count_x = const.tile([P, 1], F32)
         nc.gpsimd.memset(count_x[:], float(kinds[BILL]["d"]))
         stats = {}
@@ -305,14 +298,16 @@ def tile_featureprojector_pa_kernel(
         def invert(j, g):
             mv = mean_var[(j, g)]
             var_eps = small.tile([P, GROUP], F32, tag="var_eps")
-            nc.gpsimd.tensor_scalar(out=var_eps[:], in0=mv[:, :, 1], scalar1=1.0, scalar2=LN_EPS, op0=ALU.mult, op1=ALU.add)
+            nc.vector.tensor_scalar(out=var_eps[:], in0=mv[:, :, 1], scalar1=LN_EPS, scalar2=None, op0=ALU.add)
             scale = small.tile([P, GROUP], F32, tag="scale")
             nc.gpsimd.tensor_tensor(out=scale[:], in0=var_eps[:], in1=neg_half[:], op=ALU.pow)
-            neg_mean = small.tile([P, GROUP], F32, tag="neg_mean")
-            nc.gpsimd.tensor_scalar(out=neg_mean[:], in0=mv[:, :, 0], scalar1=-1.0, scalar2=0.0, op0=ALU.mult, op1=ALU.add)
-            shift = small.tile([P, GROUP], F32, tag="shift")
-            nc.gpsimd.tensor_tensor(out=shift[:], in0=neg_mean[:], in1=scale[:], op=ALU.mult)
             row_scale[(j, g)] = scale
+
+        def shift_rows(j, g):
+            shift = small.tile([P, GROUP], F32, tag="shift")
+            nc.vector.scalar_tensor_tensor(
+                out=shift[:], in0=mean_var[(j, g)][:, :, 0], scalar=-1.0, in1=row_scale[(j, g)][:], op0=ALU.mult, op1=ALU.mult
+            )
             row_shift[(j, g)] = shift
 
         def normalise(u, vector_tiles):
@@ -334,13 +329,12 @@ def tile_featureprojector_pa_kernel(
                     )
             if is_last:
                 for i in range(GROUP):
-                    nc.gpsimd.tensor_scalar(
+                    nc.scalar.activation(
                         out=xn[:, i, :, width:P],
-                        in0=last[:, j, g * GROUP + i, :].rearrange("r (p t) -> r t p", t=PACK),
-                        scalar1=scale[:, i : i + 1],
-                        scalar2=shift[:, i : i + 1],
-                        op0=ALU.mult,
-                        op1=ALU.add,
+                        in_=last[:, j, g * GROUP + i, :].rearrange("r (p t) -> r t p", t=PACK),
+                        func=ACT.Identity,
+                        scale=scale[:, i : i + 1],
+                        bias=shift[:, i : i + 1],
                     )
             normalised[u] = xn
 
@@ -448,6 +442,12 @@ def tile_featureprojector_pa_kernel(
                 aggregate(j, g)
                 invert(j, g)
 
+        def weave(*chains):
+            for k in range(max(len(chain) for chain in chains)):
+                for chain in chains:
+                    if k < len(chain):
+                        chain[k]()
+
         def run(steps):
             for step in steps:
                 step()
@@ -458,52 +458,43 @@ def tile_featureprojector_pa_kernel(
         def vector_planes(u):
             return 0 if u < n_units - LATE else VECTOR_PLANES_LATE
 
-        with tc.manual_schedule():
+        with tc.manual_schedule(engines={mybir.EngineType.PE, mybir.EngineType.SP}):
             nc.scalar.copy(out=b0_f32[:], in_=b_sb[:, 0:1])
-            bill_phase = phase_steps(BILL, nc.vector)
-            version_phase = phase_steps(VERSION, nc.gpsimd)
+            bill_phase = phase_steps(BILL, nc.vector) + [lambda: limit_phase(BILL)]
+            version_phase = phase_steps(VERSION, nc.vector) + [lambda: limit_phase(VERSION)]
             open_statistics(0)
             rows = statistics_steps(0)
             new_stats(*groups[1])
             rows_1 = statistics_steps(1)
-            run(bill_phase[:2])
-            for k in range(2, 5):
-                bill_phase[k]()
-                rows[k - 2]()
-            bill_phase[5]()
-            rows_1[0]()
-            limit_phase(BILL)
-            scalar_statistics(*groups[0], scalar_rows[groups[0]])
+            weave(bill_phase[:2], version_phase[:2])
+            weave(bill_phase[2:], rows[:-1] + version_phase[2:3])
             nc.scalar.copy(out=w0_f32[:], in_=w0_sb[:])
+            weave(version_phase[3:], rows_1[:-1])
             time_features(BILL)
             turn_gamma_beta()
-            run(version_phase[:3])
             rows[-1]()
             end_of_x(*groups[1])
-            scalar_statistics(*groups[1], scalar_rows[groups[1]][:1])
             close_statistics(0)
             open_statistics(2)
             rows_1[-1]()
             rows_2 = statistics_steps(2)
             rows_2[0]()
-            normalise(0, 2)
-            scalar_statistics(*groups[1], scalar_rows[groups[1]][1:])
-            turn(0)
-            run(version_phase[3:])
-            limit_phase(VERSION)
-            close_statistics(1)
             rows_2[1]()
+            shift_rows(*groups[0])
+            normalise(0, 2)
+            turn(0)
+            close_statistics(1)
             time_features(VERSION)
             rows_2[2]()
+            shift_rows(*groups[1])
             normalise(1, 1)
-            interleave_w(0)
+            for c in range(all_passes):
+                interleave_w(c)
             run(statistics_steps(3))
             for s in range(n_units + 2):
                 k = s + LOOKAHEAD
                 if k - 1 < n_units:
                     close_statistics(k - 1)
-                if s in (0, 2):
-                    interleave_w(1 + s // 2)
                 if s < n_units:
                     leave(s, vector_planes(s), whole)
                 for later in [k, k + 1] if s == 0 else [k + 1]:
@@ -514,6 +505,8 @@ def tile_featureprojector_pa_kernel(
                 if 0 <= s - 1 < n_units:
                     interleave(s - 1, whole)
                 run(steps[-1:])
+                if k - 1 < n_units and pieces[k - 1][4]:
+                    shift_rows(*pieces[k - 1][:2])
                 if 0 <= s - 2 and last_pass(s - 2):
                     gelu_and_store(s - 2, both)
                 if s == 1:

@@ -36,10 +36,10 @@ TWO_PI_HIGH = 6.28125
 TWO_PI_LOW = 2.0 * math.pi - TWO_PI_HIGH
 SIN_LIMIT = 3.1415925
 
-VECTOR_NORM_TILES = 2
+VECTOR_NORM_TILES = 1
 VECTOR_NORM_TILES_LATE = 2
 VECTOR_PLANES_LATE = 1
-LATE = 3
+LATE = 4
 LOOKAHEAD = 4
 
 FLOPS = 2 * ROWS * D_OUT * (512 + 1024)
@@ -134,6 +134,9 @@ def tile_featureprojector_pa_kernel(
         for j, g in groups[3:]:
             load_rows(j, g)
 
+        zero = const.tile([P, 1], F32)
+        nc.vector.memset(zero[:], 0.0)
+        warm = const.tile([P, 1], F32)
         identity = const.tile([P, P], F32)
         make_identity(nc, identity[:])
         neg_half = const.tile([P, GROUP], F32)
@@ -225,7 +228,7 @@ def tile_featureprojector_pa_kernel(
                 in_=w_grouped[:, c, :, :].rearrange("p n t -> p (n t)"),
             )
 
-        scalar_rows = {}
+        scalar_rows = {groups[0]: [3], groups[1]: [3]}
         count_x = const.tile([P, 1], F32)
         nc.gpsimd.memset(count_x[:], float(kinds[BILL]["d"]))
         stats = {}
@@ -298,10 +301,23 @@ def tile_featureprojector_pa_kernel(
         def invert(j, g):
             mv = mean_var[(j, g)]
             var_eps = small.tile([P, GROUP], F32, tag="var_eps")
-            nc.vector.tensor_scalar(out=var_eps[:], in0=mv[:, :, 1], scalar1=LN_EPS, scalar2=None, op0=ALU.add)
             scale = small.tile([P, GROUP], F32, tag="scale")
+            if (j, g) in groups[:2]:
+                nc.vector.tensor_scalar(out=var_eps[:], in0=mv[:, :, 1], scalar1=LN_EPS, scalar2=None, op0=ALU.add)
+            else:
+                nc.gpsimd.tensor_scalar(
+                    out=var_eps[:], in0=mv[:, :, 1], scalar1=1.0, scalar2=LN_EPS, op0=ALU.mult, op1=ALU.add
+                )
             nc.gpsimd.tensor_tensor(out=scale[:], in0=var_eps[:], in1=neg_half[:], op=ALU.pow)
             row_scale[(j, g)] = scale
+            if (j, g) not in groups[:2]:
+                neg_mean = small.tile([P, GROUP], F32, tag="neg_mean")
+                nc.gpsimd.tensor_scalar(
+                    out=neg_mean[:], in0=mv[:, :, 0], scalar1=-1.0, scalar2=0.0, op0=ALU.mult, op1=ALU.add
+                )
+                shift = small.tile([P, GROUP], F32, tag="shift")
+                nc.gpsimd.tensor_tensor(out=shift[:], in0=neg_mean[:], in1=scale[:], op=ALU.mult)
+                row_shift[(j, g)] = shift
 
         def shift_rows(j, g):
             shift = small.tile([P, GROUP], F32, tag="shift")
@@ -455,67 +471,81 @@ def tile_featureprojector_pa_kernel(
         def vector_norm(u):
             return VECTOR_NORM_TILES if u < n_units - LATE else VECTOR_NORM_TILES_LATE
 
+        def column_parts(u):
+            half = GROUP_COLS // 2
+            return [slice(0, half), slice(half, GROUP_COLS)] if u == n_units - 1 else [whole]
+
         def vector_planes(u):
             return 0 if u < n_units - LATE else VECTOR_PLANES_LATE
 
-        with tc.manual_schedule(engines={mybir.EngineType.PE, mybir.EngineType.SP}):
+        with tc.manual_schedule():
+            nc.scalar.activation(out=warm[:], in_=zero[:], func=ACT.Sin)
             nc.scalar.copy(out=b0_f32[:], in_=b_sb[:, 0:1])
             bill_phase = phase_steps(BILL, nc.vector) + [lambda: limit_phase(BILL)]
             version_phase = phase_steps(VERSION, nc.vector) + [lambda: limit_phase(VERSION)]
             open_statistics(0)
             rows = statistics_steps(0)
-            new_stats(*groups[1])
+            open_statistics(1)
             rows_1 = statistics_steps(1)
-            weave(bill_phase[:2], version_phase[:2])
-            weave(bill_phase[2:], rows[:-1] + version_phase[2:3])
+            weave(bill_phase[:3], version_phase[:3])
+            weave(bill_phase[3:], rows[:-1])
+            scalar_statistics(*groups[0], scalar_rows[groups[0]])
             nc.scalar.copy(out=w0_f32[:], in_=w0_sb[:])
-            weave(version_phase[3:], rows_1[:-1])
             time_features(BILL)
             turn_gamma_beta()
+            weave(version_phase[3:5], rows_1[:1])
             rows[-1]()
-            end_of_x(*groups[1])
+            scalar_statistics(*groups[1], scalar_rows[groups[1]][:1])
             close_statistics(0)
+            weave(version_phase[5:], rows_1[1:-1])
             open_statistics(2)
-            rows_1[-1]()
             rows_2 = statistics_steps(2)
-            rows_2[0]()
-            rows_2[1]()
             shift_rows(*groups[0])
             normalise(0, 2)
             turn(0)
+            scalar_statistics(*groups[1], scalar_rows[groups[1]][1:])
+            for c in [0]:
+                interleave_w(c)
+            rows_1[-1]()
+            rows_2[0]()
             close_statistics(1)
             time_features(VERSION)
-            rows_2[2]()
+            nc.scalar.activation(out=warm[:], in_=zero[:], func=ACT.Gelu)
+            rows_2[1]()
             shift_rows(*groups[1])
             normalise(1, 1)
-            for c in range(all_passes):
-                interleave_w(c)
+            rows_2[2]()
             run(statistics_steps(3))
             for s in range(n_units + 2):
                 k = s + LOOKAHEAD
                 if k - 1 < n_units:
                     close_statistics(k - 1)
                 if s < n_units:
-                    leave(s, vector_planes(s), whole)
+                    for cols in column_parts(s):
+                        leave(s, vector_planes(s), cols)
                 for later in [k, k + 1] if s == 0 else [k + 1]:
                     if later < n_units:
                         open_statistics(later)
                 steps = statistics_steps(k) if k < n_units else []
                 run(steps[:-1])
                 if 0 <= s - 1 < n_units:
-                    interleave(s - 1, whole)
+                    for cols in column_parts(s - 1):
+                        interleave(s - 1, cols)
                 run(steps[-1:])
-                if k - 1 < n_units and pieces[k - 1][4]:
-                    shift_rows(*pieces[k - 1][:2])
                 if 0 <= s - 2 and last_pass(s - 2):
-                    gelu_and_store(s - 2, both)
+                    for halves in [[0], [1]] if s - 2 == n_units - 1 else [both]:
+                        gelu_and_store(s - 2, halves)
+                if s == 0:
+                    for c in [1, 2]:
+                        interleave_w(c)
                 if s == 1:
                     quantise_w(0)
                 if s == 3:
                     for c in range(1, all_passes):
                         quantise_w(c)
                 if 0 <= s - 1 < n_units:
-                    quantise(s - 1, whole)
+                    for cols in column_parts(s - 1):
+                        quantise(s - 1, cols)
                 if s + 2 < n_units:
                     normalise(s + 2, vector_norm(s + 2))
                 if s + 1 < n_units:

@@ -36,7 +36,7 @@ TWO_PI_HIGH = 6.28125
 TWO_PI_LOW = 2.0 * math.pi - TWO_PI_HIGH
 SIN_LIMIT = 3.1415925
 
-VECTOR_NORM_TILES = 1
+VECTOR_NORM_TILES = 0
 VECTOR_NORM_TILES_LATE = 2
 VECTOR_PLANES_LATE = 1
 LATE = 4
@@ -301,23 +301,10 @@ def tile_featureprojector_pa_kernel(
         def invert(j, g):
             mv = mean_var[(j, g)]
             var_eps = small.tile([P, GROUP], F32, tag="var_eps")
+            nc.vector.tensor_scalar(out=var_eps[:], in0=mv[:, :, 1], scalar1=LN_EPS, scalar2=None, op0=ALU.add)
             scale = small.tile([P, GROUP], F32, tag="scale")
-            if (j, g) in groups[:2]:
-                nc.vector.tensor_scalar(out=var_eps[:], in0=mv[:, :, 1], scalar1=LN_EPS, scalar2=None, op0=ALU.add)
-            else:
-                nc.gpsimd.tensor_scalar(
-                    out=var_eps[:], in0=mv[:, :, 1], scalar1=1.0, scalar2=LN_EPS, op0=ALU.mult, op1=ALU.add
-                )
             nc.gpsimd.tensor_tensor(out=scale[:], in0=var_eps[:], in1=neg_half[:], op=ALU.pow)
             row_scale[(j, g)] = scale
-            if (j, g) not in groups[:2]:
-                neg_mean = small.tile([P, GROUP], F32, tag="neg_mean")
-                nc.gpsimd.tensor_scalar(
-                    out=neg_mean[:], in0=mv[:, :, 0], scalar1=-1.0, scalar2=0.0, op0=ALU.mult, op1=ALU.add
-                )
-                shift = small.tile([P, GROUP], F32, tag="shift")
-                nc.gpsimd.tensor_tensor(out=shift[:], in0=neg_mean[:], in1=scale[:], op=ALU.mult)
-                row_shift[(j, g)] = shift
 
         def shift_rows(j, g):
             shift = small.tile([P, GROUP], F32, tag="shift")
@@ -532,6 +519,8 @@ def tile_featureprojector_pa_kernel(
                     for cols in column_parts(s - 1):
                         interleave(s - 1, cols)
                 run(steps[-1:])
+                if k - 1 < n_units and pieces[k - 1][4]:
+                    shift_rows(*pieces[k - 1][:2])
                 if 0 <= s - 2 and last_pass(s - 2):
                     for halves in [[0], [1]] if s - 2 == n_units - 1 else [both]:
                         gelu_and_store(s - 2, halves)

@@ -36,7 +36,7 @@ TWO_PI_HIGH = 6.28125
 TWO_PI_LOW = 2.0 * math.pi - TWO_PI_HIGH
 SIN_LIMIT = 3.1415925
 
-VECTOR_NORM_TILES = 0
+VECTOR_NORM_TILES = 1
 VECTOR_NORM_TILES_LATE = 2
 VECTOR_PLANES_LATE = 1
 LATE = 4
@@ -127,8 +127,8 @@ def tile_featureprojector_pa_kernel(
         nc.sync.dma_start(out=w0_sb[:], in_=w0.partition_broadcast(P))
         for kind in kinds:
             load_gamma_beta(kind)
-        load_rows(*groups[1])
         load_w(kinds[BILL])
+        load_rows(*groups[1])
         load_rows(*groups[2])
         load_w(kinds[VERSION])
         for j, g in groups[3:]:
@@ -328,7 +328,12 @@ def tile_featureprojector_pa_kernel(
                     )
                 else:
                     nc.vector.tensor_scalar(
-                        out=dst, in0=src, scalar1=scale[:, i : i + 1], scalar2=shift[:, i : i + 1], op0=ALU.mult, op1=ALU.add
+                        out=dst,
+                        in0=src,
+                        scalar1=mean_var[(j, g)][:, i, 0:1],
+                        scalar2=scale[:, i : i + 1],
+                        op0=ALU.subtract,
+                        op1=ALU.mult,
                     )
             if is_last:
                 for i in range(GROUP):
@@ -472,14 +477,17 @@ def tile_featureprojector_pa_kernel(
             version_phase = phase_steps(VERSION, nc.vector) + [lambda: limit_phase(VERSION)]
             open_statistics(0)
             rows = statistics_steps(0)
-            open_statistics(1)
+            new_stats(*groups[1])
             rows_1 = statistics_steps(1)
             weave(bill_phase[:3], version_phase[:3])
             weave(bill_phase[3:], rows[:-1])
             scalar_statistics(*groups[0], scalar_rows[groups[0]])
             nc.scalar.copy(out=w0_f32[:], in_=w0_sb[:])
+            for c in [0]:
+                interleave_w(c)
             time_features(BILL)
             turn_gamma_beta()
+            end_of_x(*groups[1])
             weave(version_phase[3:5], rows_1[:1])
             rows[-1]()
             scalar_statistics(*groups[1], scalar_rows[groups[1]][:1])
@@ -491,7 +499,7 @@ def tile_featureprojector_pa_kernel(
             normalise(0, 2)
             turn(0)
             scalar_statistics(*groups[1], scalar_rows[groups[1]][1:])
-            for c in [0]:
+            for c in []:
                 interleave_w(c)
             rows_1[-1]()
             rows_2[0]()

@@ -22,9 +22,7 @@ GROUPS = ROW_TILES // GROUP
 GROUP_COLS = GROUP * P
 T2V = 12
 N_SIN = T2V - 1
-LAST = 32
-LAST_X = LAST - T2V
-LAST_P = LAST // PACK
+T2V_P = T2V // PACK
 D_OUT = 256
 LN_EPS = 1e-5
 BN_MAX = 512
@@ -37,8 +35,8 @@ TWO_PI_LOW = 2.0 * math.pi - TWO_PI_HIGH
 SIN_LIMIT = 3.1415925
 
 VECTOR_NORM_TILES = 1
-VECTOR_NORM_TILES_LATE = 2
-VECTOR_PLANES_LATE = 1
+VECTOR_NORM_TILES_LATE = 3
+VECTOR_PLANES_LATE = 0
 LATE = 4
 LOOKAHEAD = 4
 
@@ -142,7 +140,7 @@ def tile_featureprojector_pa_kernel(
         neg_half = const.tile([P, GROUP], F32)
         nc.gpsimd.memset(neg_half[:], -0.5)
 
-        last = const.tile([P, len(kinds), ROW_TILES, LAST], F32)
+        t2v = const.tile([P, len(kinds), ROW_TILES, T2V], F32)
         w0_f32 = const.tile([P, 1], F32)
         b0_f32 = const.tile([P, 1], F32)
         reduced = const.tile([P, len(kinds), ROW_TILES, N_SIN], F32)
@@ -189,9 +187,9 @@ def tile_featureprojector_pa_kernel(
             nc.vector.tensor_scalar(out=red, in0=red, scalar1=-SIN_LIMIT, scalar2=SIN_LIMIT, op0=ALU.max, op1=ALU.min)
 
         def time_features(j):
-            nc.scalar.activation(out=last[:, j, :, LAST_X + 1 : LAST], in_=reduced[:, j, :, :], func=ACT.Sin)
+            nc.scalar.activation(out=t2v[:, j, :, 1:T2V], in_=reduced[:, j, :, :], func=ACT.Sin)
             nc.scalar.activation(
-                out=last[:, j, :, LAST_X : LAST_X + 1],
+                out=t2v[:, j, :, 0:1],
                 in_=ts_sb[:, j, :].unsqueeze(2),
                 func=ACT.Identity,
                 scale=w0_f32[:],
@@ -243,11 +241,6 @@ def tile_featureprojector_pa_kernel(
         zn_scales = {}
         sums = {}
 
-        def end_of_x(j, g):
-            rows = slice(g * GROUP, (g + 1) * GROUP)
-            d = kinds[j]["d"]
-            nc.scalar.copy(out=last[:, j, rows, 0:LAST_X], in_=x_sb[(j, g)][:, :, d - LAST_X : d])
-
         def new_stats(j, g):
             n = 2 * (kinds[j]["chunks"] + 1)
             stats[(j, g)] = small.tile([P, GROUP, n * TRIPLE], F32, tag="stats", name="stats")
@@ -289,7 +282,7 @@ def tile_featureprojector_pa_kernel(
         def time_statistics(j, g, i):
             n = 2 * kinds[j]["chunks"]
             nc.vector.bn_stats(
-                out=stats[(j, g)][:, i, n * TRIPLE : (n + 2) * TRIPLE], in_=last[:, j, g * GROUP + i, LAST_X:LAST]
+                out=stats[(j, g)][:, i, n * TRIPLE : (n + 2) * TRIPLE], in_=t2v[:, j, g * GROUP + i, :]
             )
 
         def aggregate(j, g):
@@ -318,7 +311,7 @@ def tile_featureprojector_pa_kernel(
             scale, shift = row_scale[(j, g)], row_shift[(j, g)]
             xn = xn_pool.tile([P, GROUP, PACK, P], F32, tag="xn", name="xn")
             is_last = c == kinds[j]["passes"] - 1
-            width = P - LAST_P if is_last else P
+            width = P - T2V_P if is_last else P
             for i in range(GROUP):
                 dst = xn[:, i, :, 0:width]
                 src = x_sb[(j, g)][:, i, c * K_PASS : c * K_PASS + width * PACK].rearrange("r (p t) -> r t p", t=PACK)
@@ -339,7 +332,7 @@ def tile_featureprojector_pa_kernel(
                 for i in range(GROUP):
                     nc.scalar.activation(
                         out=xn[:, i, :, width:P],
-                        in_=last[:, j, g * GROUP + i, :].rearrange("r (p t) -> r t p", t=PACK),
+                        in_=t2v[:, j, g * GROUP + i, :].rearrange("r (p t) -> r t p", t=PACK),
                         func=ACT.Identity,
                         scale=scale[:, i : i + 1],
                         bias=shift[:, i : i + 1],
@@ -436,7 +429,6 @@ def tile_featureprojector_pa_kernel(
             j, g, tiles, is_first, is_last = pieces[k]
             if is_first:
                 new_stats(j, g)
-                end_of_x(j, g)
 
         def statistics_steps(k):
             j, g, tiles, is_first, is_last = pieces[k]
@@ -487,7 +479,6 @@ def tile_featureprojector_pa_kernel(
                 interleave_w(c)
             time_features(BILL)
             turn_gamma_beta()
-            end_of_x(*groups[1])
             weave(version_phase[3:5], rows_1[:1])
             rows[-1]()
             scalar_statistics(*groups[1], scalar_rows[groups[1]][:1])
@@ -496,7 +487,7 @@ def tile_featureprojector_pa_kernel(
             open_statistics(2)
             rows_2 = statistics_steps(2)
             shift_rows(*groups[0])
-            normalise(0, 2)
+            normalise(0, 1)
             turn(0)
             scalar_statistics(*groups[1], scalar_rows[groups[1]][1:])
             for c in []:
@@ -508,7 +499,7 @@ def tile_featureprojector_pa_kernel(
             nc.scalar.activation(out=warm[:], in_=zero[:], func=ACT.Gelu)
             rows_2[1]()
             shift_rows(*groups[1])
-            normalise(1, 1)
+            normalise(1, 0)
             rows_2[2]()
             run(statistics_steps(3))
             for s in range(n_units + 2):
@@ -522,16 +513,12 @@ def tile_featureprojector_pa_kernel(
                     if later < n_units:
                         open_statistics(later)
                 steps = statistics_steps(k) if k < n_units else []
-                run(steps[:-1])
                 if 0 <= s - 1 < n_units:
                     for cols in column_parts(s - 1):
                         interleave(s - 1, cols)
-                run(steps[-1:])
+                run(steps)
                 if k - 1 < n_units and pieces[k - 1][4]:
                     shift_rows(*pieces[k - 1][:2])
-                if 0 <= s - 2 and last_pass(s - 2):
-                    for halves in [[0], [1]] if s - 2 == n_units - 1 else [both]:
-                        gelu_and_store(s - 2, halves)
                 if s == 0:
                     for c in [1, 2]:
                         interleave_w(c)
@@ -540,11 +527,15 @@ def tile_featureprojector_pa_kernel(
                 if s == 3:
                     for c in range(1, all_passes):
                         quantise_w(c)
-                if 0 <= s - 1 < n_units:
-                    for cols in column_parts(s - 1):
-                        quantise(s - 1, cols)
+                if 0 <= s - 1 < n_units and last_pass(s - 1):
+                    for u in range(s - 1 - units[s - 1][2], s):
+                        for cols in column_parts(u):
+                            quantise(u, cols)
                 if s + 2 < n_units:
                     normalise(s + 2, vector_norm(s + 2))
+                if 0 <= s - 2 and last_pass(s - 2):
+                    for halves in [[0], [1]] if s - 2 == n_units - 1 else [both]:
+                        gelu_and_store(s - 2, halves)
                 if s + 1 < n_units:
                     turn(s + 1)
                 if 0 <= s - 1 < n_units and last_pass(s - 1):

@@ -34,10 +34,6 @@ TWO_PI_HIGH = 6.28125
 TWO_PI_LOW = 2.0 * math.pi - TWO_PI_HIGH
 SIN_LIMIT = 3.1415925
 
-VECTOR_NORM_TILES = 1
-VECTOR_NORM_TILES_LATE = 3
-VECTOR_PLANES_LATE = 0
-LATE = 4
 LOOKAHEAD = 4
 
 FLOPS = 2 * ROWS * D_OUT * (512 + 1024)
@@ -127,9 +123,8 @@ def tile_featureprojector_pa_kernel(
             load_gamma_beta(kind)
         load_w(kinds[BILL])
         load_rows(*groups[1])
-        load_rows(*groups[2])
         load_w(kinds[VERSION])
-        for j, g in groups[3:]:
+        for j, g in groups[2:]:
             load_rows(j, g)
 
         zero = const.tile([P, 1], F32)
@@ -145,46 +140,37 @@ def tile_featureprojector_pa_kernel(
         b0_f32 = const.tile([P, 1], F32)
         reduced = const.tile([P, len(kinds), ROW_TILES, N_SIN], F32)
 
-        def phase_steps(j, engine):
+        def phase_steps(j):
             shape = [P, ROW_TILES, N_SIN]
             phase = const.tile(shape, F32, name="phase_%d" % j)
             turns = const.tile(shape, F32, name="turns_%d" % j)
-            part = const.tile(shape, F32, name="part_%d" % j)
             red = reduced[:, j, :, :]
-            by_vector = engine is nc.vector
             ts_wide = ts_sb[:, j, :].unsqueeze(2).to_broadcast(shape)
             w_wide = w_sb[:].unsqueeze(1).to_broadcast(shape)
             b_wide = b_sb[:, 1:T2V].unsqueeze(1).to_broadcast(shape)
 
             def tensor(dst, in0, in1, op):
-                return lambda: engine.tensor_tensor(out=dst, in0=in0, in1=in1, op=op)
+                return lambda: nc.vector.tensor_tensor(out=dst, in0=in0, in1=in1, op=op)
 
-            def affine(dst, in0, factor, term):
-                return lambda: engine.tensor_scalar(
-                    out=dst, in0=in0, scalar1=factor, scalar2=term, op0=ALU.mult, op1=ALU.add
+            def scalar(dst, in0, scalar1, scalar2, op0, op1):
+                return lambda: nc.vector.tensor_scalar(
+                    out=dst, in0=in0, scalar1=scalar1, scalar2=scalar2, op0=op0, op1=op1
                 )
 
             def take_off(dst, src, two_pi):
-                if by_vector:
-                    return [
-                        lambda: nc.vector.scalar_tensor_tensor(
-                            out=dst, in0=turns[:], scalar=-two_pi, in1=src, op0=ALU.mult, op1=ALU.add
-                        )
-                    ]
-                return [affine(part[:], turns[:], -two_pi, 0.0), tensor(dst, src, part[:], ALU.add)]
+                return lambda: nc.vector.scalar_tensor_tensor(
+                    out=dst, in0=turns[:], scalar=-two_pi, in1=src, op0=ALU.mult, op1=ALU.add
+                )
 
             return [
                 tensor(phase[:], ts_wide, w_wide, ALU.mult),
                 tensor(phase[:], phase[:], b_wide, ALU.add),
-                affine(turns[:], phase[:], 1.0 / (2.0 * math.pi), ROUND_MAGIC),
-                affine(turns[:], turns[:], 1.0, -ROUND_MAGIC),
-                *take_off(red, phase[:], TWO_PI_HIGH),
-                *take_off(red, red, TWO_PI_LOW),
+                scalar(turns[:], phase[:], 1.0 / (2.0 * math.pi), ROUND_MAGIC, ALU.mult, ALU.add),
+                scalar(turns[:], turns[:], 1.0, -ROUND_MAGIC, ALU.mult, ALU.add),
+                take_off(red, phase[:], TWO_PI_HIGH),
+                take_off(red, red, TWO_PI_LOW),
+                scalar(red, red, -SIN_LIMIT, SIN_LIMIT, ALU.max, ALU.min),
             ]
-
-        def limit_phase(j):
-            red = reduced[:, j, :, :]
-            nc.vector.tensor_scalar(out=red, in0=red, scalar1=-SIN_LIMIT, scalar2=SIN_LIMIT, op0=ALU.max, op1=ALU.min)
 
         def time_features(j):
             nc.scalar.activation(out=t2v[:, j, :, 1:T2V], in_=reduced[:, j, :, :], func=ACT.Sin)
@@ -226,9 +212,7 @@ def tile_featureprojector_pa_kernel(
                 in_=w_grouped[:, c, :, :].rearrange("p n t -> p (n t)"),
             )
 
-        scalar_rows = {groups[0]: [3], groups[1]: [3]}
-        count_x = const.tile([P, 1], F32)
-        nc.gpsimd.memset(count_x[:], float(kinds[BILL]["d"]))
+        scalar_tile = GROUP - 1
         stats = {}
         mean_var = {}
         row_scale = {}
@@ -241,9 +225,17 @@ def tile_featureprojector_pa_kernel(
         zn_scales = {}
         sums = {}
 
+        def by_scalar(j, g, i):
+            return (j, g) in groups[:2] and i == scalar_tile
+
         def new_stats(j, g):
-            n = 2 * (kinds[j]["chunks"] + 1)
-            stats[(j, g)] = small.tile([P, GROUP, n * TRIPLE], F32, tag="stats", name="stats")
+            n = 2 * (kinds[j]["chunks"] + 1) * TRIPLE
+            st = const.tile([P, GROUP, n + TRIPLE], F32, name="stats_%d_%d" % (j, g))
+            nc.vector.memset(st[:, :, n : n + 2], 0.0)
+            nc.vector.memset(st[:, :, n + 2 : n + TRIPLE], LN_EPS * kinds[j]["passes"] * K_PASS)
+            if by_scalar(j, g, scalar_tile):
+                nc.vector.memset(st[:, scalar_tile, TRIPLE : TRIPLE + 1], float(kinds[j]["d"]))
+            stats[(j, g)] = st
 
         def row_statistics(j, g, i):
             chunks = kinds[j]["chunks"]
@@ -254,30 +246,16 @@ def tile_featureprojector_pa_kernel(
                     in_=x_sb[(j, g)][:, i, h * width : (h + 1) * width],
                 )
 
-        def scalar_statistics(j, g, tiles):
-            d = kinds[j]["d"]
+        def scalar_statistics(j, g):
+            i, d = scalar_tile, kinds[j]["d"]
             junk = small.tile([P, d], BF16, tag="junk", name="junk")
-            neg_mean = small.tile([P, GROUP], F32, tag="minus", name="minus")
-            st = stats[(j, g)]
-            for i in tiles:
-                nc.scalar.activation(
-                    out=junk[:],
-                    in_=x_sb[(j, g)][:, i, :],
-                    func=ACT.Copy,
-                    scale=1.0 / d,
-                    accum_out=st[:, i, TRIPLE + 1 : TRIPLE + 2],
-                )
-            for i in tiles:
-                nc.scalar.mul(neg_mean[:, i : i + 1], st[:, i, TRIPLE + 1 : TRIPLE + 2], -1.0)
-                nc.scalar.copy(out=st[:, i, TRIPLE : TRIPLE + 1], in_=count_x[:])
-            for i in tiles:
-                nc.scalar.activation(
-                    out=junk[:],
-                    in_=x_sb[(j, g)][:, i, :],
-                    func=ACT.Square,
-                    bias=neg_mean[:, i : i + 1],
-                    accum_out=st[:, i, TRIPLE + 2 : TRIPLE + 3],
-                )
+            neg_mean = small.tile([P, 1], F32, tag="neg_mean", name="neg_mean")
+            row, triple = x_sb[(j, g)][:, i, :], stats[(j, g)][:, i, TRIPLE : 2 * TRIPLE]
+            nc.scalar.activation(out=junk[:], in_=row, func=ACT.Copy, scale=-1.0 / d, accum_out=neg_mean[:])
+            nc.scalar.activation(
+                out=junk[:], in_=row, func=ACT.Square, bias=neg_mean[:], accum_out=triple[:, 2:3]
+            )
+            nc.scalar.mul(triple[:, 1:2], neg_mean[:], -1.0)
 
         def time_statistics(j, g, i):
             n = 2 * kinds[j]["chunks"]
@@ -288,15 +266,12 @@ def tile_featureprojector_pa_kernel(
         def aggregate(j, g):
             mean_var[(j, g)] = small.tile([P, GROUP, 2], F32, tag="mean_var", name="mean_var")
             for i in range(GROUP):
-                start = TRIPLE if i in scalar_rows.get((j, g), ()) else 0
+                start = TRIPLE if by_scalar(j, g, i) else 0
                 nc.vector.bn_aggr(out=mean_var[(j, g)][:, i, :], in_=stats[(j, g)][:, i, start:])
 
         def invert(j, g):
-            mv = mean_var[(j, g)]
-            var_eps = small.tile([P, GROUP], F32, tag="var_eps")
-            nc.vector.tensor_scalar(out=var_eps[:], in0=mv[:, :, 1], scalar1=LN_EPS, scalar2=None, op0=ALU.add)
             scale = small.tile([P, GROUP], F32, tag="scale")
-            nc.gpsimd.tensor_tensor(out=scale[:], in0=var_eps[:], in1=neg_half[:], op=ALU.pow)
+            nc.gpsimd.tensor_tensor(out=scale[:], in0=mean_var[(j, g)][:, :, 1], in1=neg_half[:], op=ALU.pow)
             row_scale[(j, g)] = scale
 
         def shift_rows(j, g):
@@ -346,19 +321,18 @@ def tile_featureprojector_pa_kernel(
                     nc.tensor.transpose(bank[:, i * P : (i + 1) * P], normalised[u][:, i, t, :], identity[:])
                 banks[(u, t)] = bank
 
-        def leave(u, vector_planes, cols):
+        def leave(u):
             j, g, c = units[u]
-            if u not in planes:
-                planes[u] = work.tile([P, PACK, GROUP_COLS], BF16, tag="planes", name="planes")
+            planes[u] = work.tile([P, PACK, GROUP_COLS], BF16, tag="planes", name="planes")
             col = kinds[j]["first"] + c
             for t in range(PACK):
-                scale = gamma_beta[:, t, col : col + 1]
-                bias = gamma_beta[:, t, all_passes + col : all_passes + col + 1]
-                dst, src = planes[u][:, t, cols], banks[(u, t)][:, cols]
-                if t < PACK - vector_planes:
-                    nc.scalar.activation(out=dst, in_=src, func=ACT.Identity, scale=scale, bias=bias)
-                else:
-                    nc.vector.tensor_scalar(out=dst, in0=src, scalar1=scale, scalar2=bias, op0=ALU.mult, op1=ALU.add)
+                nc.scalar.activation(
+                    out=planes[u][:, t, :],
+                    in_=banks[(u, t)][:],
+                    func=ACT.Identity,
+                    scale=gamma_beta[:, t, col : col + 1],
+                    bias=gamma_beta[:, t, all_passes + col : all_passes + col + 1],
+                )
 
         def interleave(u, cols):
             if u not in grouped:
@@ -378,10 +352,10 @@ def tile_featureprojector_pa_kernel(
                 in_=grouped[u][:, cols, :].rearrange("p n t -> p (n t)"),
             )
 
-        def multiply(u, halves):
+        def multiply(u):
             j, g, c = units[u]
             passes = c + 1
-            for half in halves:
+            for half in range(2):
                 acc = acc_pool.tile([P, 2, D_OUT], F32, tag="acc", name="acc")
                 for s in range(2):
                     i = half * 2 + s
@@ -415,32 +389,25 @@ def tile_featureprojector_pa_kernel(
         for j, g in groups:
             n = kinds[j]["passes"]
             for c in range(n):
-                pieces.append((j, g, range(c * GROUP // n, (c + 1) * GROUP // n), c == 0, c == n - 1))
+                pieces.append((j, g, range(c * GROUP // n, (c + 1) * GROUP // n), c == n - 1))
 
-        whole = slice(0, GROUP_COLS)
-        both = [0, 1]
         n_units = len(units)
 
-        def last_pass(u):
+        def is_last_pass(u):
             j, g, c = units[u]
             return c == kinds[j]["passes"] - 1
 
-        def open_statistics(k):
-            j, g, tiles, is_first, is_last = pieces[k]
-            if is_first:
-                new_stats(j, g)
+        def x_steps(k):
+            j, g, tiles, ends_group = pieces[k]
+            return [lambda i=i: row_statistics(j, g, i) for i in tiles if not by_scalar(j, g, i)]
 
-        def statistics_steps(k):
-            j, g, tiles, is_first, is_last = pieces[k]
-            steps = [lambda i=i: row_statistics(j, g, i) for i in tiles if i not in scalar_rows.get((j, g), ())]
-            steps.append(lambda: [time_statistics(j, g, i) for i in tiles])
-            return steps
+        def time_steps(k):
+            j, g, tiles, ends_group = pieces[k]
+            return [lambda i=i: time_statistics(j, g, i) for i in tiles]
 
-        def close_statistics(k):
-            j, g, tiles, is_first, is_last = pieces[k]
-            if is_last:
-                aggregate(j, g)
-                invert(j, g)
+        def run(steps):
+            for step in steps:
+                step()
 
         def weave(*chains):
             for k in range(max(len(chain) for chain in chains)):
@@ -448,95 +415,85 @@ def tile_featureprojector_pa_kernel(
                     if k < len(chain):
                         chain[k]()
 
-        def run(steps):
-            for step in steps:
-                step()
-
-        def vector_norm(u):
-            return VECTOR_NORM_TILES if u < n_units - LATE else VECTOR_NORM_TILES_LATE
+        def vector_tiles(u):
+            if u < 2:
+                return 0
+            return 1 if u + LOOKAHEAD <= n_units else GROUP
 
         def column_parts(u):
             half = GROUP_COLS // 2
-            return [slice(0, half), slice(half, GROUP_COLS)] if u == n_units - 1 else [whole]
-
-        def vector_planes(u):
-            return 0 if u < n_units - LATE else VECTOR_PLANES_LATE
+            return [slice(0, half), slice(half, GROUP_COLS)] if u == n_units - 1 else [slice(0, GROUP_COLS)]
 
         with tc.manual_schedule():
             nc.scalar.activation(out=warm[:], in_=zero[:], func=ACT.Sin)
             nc.scalar.copy(out=b0_f32[:], in_=b_sb[:, 0:1])
-            bill_phase = phase_steps(BILL, nc.vector) + [lambda: limit_phase(BILL)]
-            version_phase = phase_steps(VERSION, nc.vector) + [lambda: limit_phase(VERSION)]
-            open_statistics(0)
-            rows = statistics_steps(0)
-            new_stats(*groups[1])
-            rows_1 = statistics_steps(1)
+            for group in groups:
+                new_stats(*group)
+            bill_phase, version_phase = phase_steps(BILL), phase_steps(VERSION)
+            second_x = x_steps(1)
             weave(bill_phase[:3], version_phase[:3])
-            weave(bill_phase[3:], rows[:-1])
-            scalar_statistics(*groups[0], scalar_rows[groups[0]])
+            weave(bill_phase[3:], x_steps(0))
+            scalar_statistics(*groups[0])
             nc.scalar.copy(out=w0_f32[:], in_=w0_sb[:])
-            for c in [0]:
-                interleave_w(c)
+            interleave_w(0)
             time_features(BILL)
             turn_gamma_beta()
-            weave(version_phase[3:5], rows_1[:1])
-            rows[-1]()
-            scalar_statistics(*groups[1], scalar_rows[groups[1]][:1])
-            close_statistics(0)
-            weave(version_phase[5:], rows_1[1:-1])
-            open_statistics(2)
-            rows_2 = statistics_steps(2)
+            weave(version_phase[3:5], second_x[:1])
+            run(time_steps(0))
+            scalar_statistics(*groups[1])
+            aggregate(*groups[0])
+            invert(*groups[0])
+            interleave_w(1)
+            weave(version_phase[5:], second_x[1:])
             shift_rows(*groups[0])
-            normalise(0, 1)
+            normalise(0, vector_tiles(0))
             turn(0)
-            scalar_statistics(*groups[1], scalar_rows[groups[1]][1:])
-            for c in []:
-                interleave_w(c)
-            rows_1[-1]()
-            rows_2[0]()
-            close_statistics(1)
+            run(time_steps(1))
+            third_x = x_steps(2)
+            run(third_x[:1])
+            aggregate(*groups[1])
+            invert(*groups[1])
             time_features(VERSION)
             nc.scalar.activation(out=warm[:], in_=zero[:], func=ACT.Gelu)
-            rows_2[1]()
+            run(third_x[1:])
             shift_rows(*groups[1])
-            normalise(1, 0)
-            rows_2[2]()
-            run(statistics_steps(3))
+            normalise(1, vector_tiles(1))
+            run(time_steps(2))
+            run(x_steps(3))
+            run(time_steps(3))
             for s in range(n_units + 2):
                 k = s + LOOKAHEAD
-                if k - 1 < n_units:
-                    close_statistics(k - 1)
+                closes = k - 1 < n_units and pieces[k - 1][3]
+                multiplies = 0 <= s - 1 < n_units and is_last_pass(s - 1)
+                if closes:
+                    aggregate(*pieces[k - 1][:2])
+                    invert(*pieces[k - 1][:2])
                 if s < n_units:
-                    for cols in column_parts(s):
-                        leave(s, vector_planes(s), cols)
-                for later in [k, k + 1] if s == 0 else [k + 1]:
-                    if later < n_units:
-                        open_statistics(later)
-                steps = statistics_steps(k) if k < n_units else []
+                    leave(s)
                 if 0 <= s - 1 < n_units:
                     for cols in column_parts(s - 1):
                         interleave(s - 1, cols)
-                run(steps)
-                if k - 1 < n_units and pieces[k - 1][4]:
+                if k < n_units:
+                    run(x_steps(k))
+                    run(time_steps(k))
+                if closes:
                     shift_rows(*pieces[k - 1][:2])
                 if s == 0:
-                    for c in [1, 2]:
-                        interleave_w(c)
-                if s == 1:
+                    interleave_w(2)
                     quantise_w(0)
-                if s == 3:
-                    for c in range(1, all_passes):
-                        quantise_w(c)
-                if 0 <= s - 1 < n_units and last_pass(s - 1):
+                if s == 2:
+                    quantise_w(1)
+                    quantise_w(2)
+                if multiplies:
                     for u in range(s - 1 - units[s - 1][2], s):
                         for cols in column_parts(u):
                             quantise(u, cols)
                 if s + 2 < n_units:
-                    normalise(s + 2, vector_norm(s + 2))
-                if 0 <= s - 2 and last_pass(s - 2):
-                    for halves in [[0], [1]] if s - 2 == n_units - 1 else [both]:
+                    normalise(s + 2, vector_tiles(s + 2))
+                if 0 <= s - 2 and is_last_pass(s - 2):
+                    for halves in [[0], [1]] if s - 2 == n_units - 1 else [[0, 1]]:
                         gelu_and_store(s - 2, halves)
                 if s + 1 < n_units:
                     turn(s + 1)
-                if 0 <= s - 1 < n_units and last_pass(s - 1):
-                    multiply(s - 1, both)
+                if multiplies:
+                    multiply(s - 1)

from contextlib import ExitStack
import math

import concourse.mybir as mybir
from concourse.masks import make_identity

F32 = mybir.dt.float32
BF16 = mybir.dt.bfloat16
U32 = mybir.dt.uint32
U8 = mybir.dt.uint8
FP8X4 = mybir.dt.float8_e4m3fn_x4
ACT = mybir.ActivationFunctionType
ALU = mybir.AluOpType

P = 128
PACK = 4
K_PASS = P * PACK
ROWS = 2048
ROW_TILES = ROWS // P
GROUP = 4
GROUPS = ROW_TILES // GROUP
GROUP_COLS = GROUP * P
T2V = 12
N_SIN = T2V - 1
T2V_P = T2V // PACK
D_OUT = 256
LN_EPS = 1e-5
BN_MAX = 512
TRIPLE = 3
BILL, VERSION = 0, 1

ROUND_MAGIC = 12582912.0
TWO_PI_HIGH = 6.28125
TWO_PI_LOW = 2.0 * math.pi - TWO_PI_HIGH
SIN_LIMIT = 3.1415925

LOOKAHEAD = 4

FLOPS = 2 * ROWS * D_OUT * (512 + 1024)


def tile_featureprojector_pa_kernel(
    tc,
    x_bill,
    ts_bill,
    x_bill_version,
    ts_bill_version,
    w0,
    w,
    b,
    gamma_bill,
    beta_bill,
    W_bill,
    gamma_bill_version,
    beta_bill_version,
    W_bill_version,
    out,
):
    nc = tc.nc
    kinds = [
        {"x": x_bill, "ts": ts_bill, "gamma": gamma_bill, "beta": beta_bill, "W": W_bill, "first": 0},
        {
            "x": x_bill_version,
            "ts": ts_bill_version,
            "gamma": gamma_bill_version,
            "beta": beta_bill_version,
            "W": W_bill_version,
            "first": 1,
        },
    ]
    for kind in kinds:
        kind["d"] = kind["x"].shape[1]
        kind["passes"] = (kind["d"] + T2V) // K_PASS
        kind["chunks"] = (kind["d"] + BN_MAX - 1) // BN_MAX
    all_passes = sum(kind["passes"] for kind in kinds)

    groups = [(BILL, 0), (BILL, 1)] + [(VERSION, g) for g in range(GROUPS)] + [(BILL, 2), (BILL, 3)]
    units = [(j, g, c) for j, g in groups for c in range(kinds[j]["passes"])]

    with ExitStack() as stack:
        const = stack.enter_context(tc.tile_pool(name="const", bufs=1))
        x_pool = stack.enter_context(tc.tile_pool(name="x", bufs=1))
        small = stack.enter_context(tc.tile_pool(name="small", bufs=4))
        xn_pool = stack.enter_context(tc.tile_pool(name="xn", bufs=3))
        work = stack.enter_context(tc.tile_pool(name="work", bufs=4))
        turned_pool = stack.enter_context(tc.psum_pool(name="turned", bufs=6))
        acc_pool = stack.enter_context(tc.psum_pool(name="acc", bufs=2))

        ts_sb = const.tile([P, len(kinds), ROW_TILES], BF16)
        for j, kind in enumerate(kinds):
            nc.sync.dma_start(out=ts_sb[:, j, :], in_=kind["ts"].rearrange("(p i) -> p i", i=ROW_TILES))
        w_sb = const.tile([P, N_SIN], BF16)
        nc.sync.dma_start(out=w_sb[:], in_=w.partition_broadcast(P))
        b_sb = const.tile([P, T2V], BF16)
        nc.sync.dma_start(out=b_sb[:], in_=b.partition_broadcast(P))

        x_sb = {}

        def load_rows(j, g):
            x_tile = x_pool.tile([P, GROUP, kinds[j]["d"]], BF16, name="x_%d_%d" % (j, g))
            rows = kinds[j]["x"].rearrange("(p i) d -> p i d", i=ROW_TILES)
            nc.sync.dma_start(out=x_tile[:], in_=rows[:, g * GROUP : (g + 1) * GROUP, :])
            x_sb[(j, g)] = x_tile

        gb_rows = const.tile([P, K_PASS], BF16)
        nc.gpsimd.memset(gb_rows[:], 0.0)
        w_raw = const.tile([P, all_passes, PACK, D_OUT], BF16)

        def load_gamma_beta(kind):
            first, passes = kind["first"], kind["passes"]
            for row, name in ((first, "gamma"), (all_passes + first, "beta")):
                nc.sync.dma_start(out=gb_rows[row : row + passes, :], in_=kind[name].rearrange("(c k) -> c k", k=K_PASS))

        def load_w(kind):
            for c in range(kind["passes"]):
                rows = kind["W"][c * K_PASS : (c + 1) * K_PASS, :]
                nc.sync.dma_start(out=w_raw[:, kind["first"] + c, :, :], in_=rows.rearrange("(p t) n -> p t n", t=PACK))

        load_rows(*groups[0])
        w0_sb = const.tile([P, 1], BF16)
        nc.sync.dma_start(out=w0_sb[:], in_=w0.partition_broadcast(P))
        for kind in kinds:
            load_gamma_beta(kind)
        load_w(kinds[BILL])
        load_rows(*groups[1])
        load_w(kinds[VERSION])
        for j, g in groups[2:]:
            load_rows(j, g)

        zero = const.tile([P, 1], F32)
        nc.vector.memset(zero[:], 0.0)
        warm = const.tile([P, 1], F32)
        identity = const.tile([P, P], F32)
        make_identity(nc, identity[:])
        neg_half = const.tile([P, GROUP], F32)
        nc.gpsimd.memset(neg_half[:], -0.5)

        t2v = const.tile([P, len(kinds), ROW_TILES, T2V], F32)
        w0_f32 = const.tile([P, 1], F32)
        b0_f32 = const.tile([P, 1], F32)
        reduced = const.tile([P, len(kinds), ROW_TILES, N_SIN], F32)

        def phase_steps(j):
            shape = [P, ROW_TILES, N_SIN]
            phase = const.tile(shape, F32, name="phase_%d" % j)
            turns = const.tile(shape, F32, name="turns_%d" % j)
            red = reduced[:, j, :, :]
            ts_wide = ts_sb[:, j, :].unsqueeze(2).to_broadcast(shape)
            w_wide = w_sb[:].unsqueeze(1).to_broadcast(shape)
            b_wide = b_sb[:, 1:T2V].unsqueeze(1).to_broadcast(shape)

            def tensor(dst, in0, in1, op):
                return lambda: nc.vector.tensor_tensor(out=dst, in0=in0, in1=in1, op=op)

            def scalar(dst, in0, scalar1, scalar2, op0, op1):
                return lambda: nc.vector.tensor_scalar(
                    out=dst, in0=in0, scalar1=scalar1, scalar2=scalar2, op0=op0, op1=op1
                )

            def take_off(dst, src, two_pi):
                return lambda: nc.vector.scalar_tensor_tensor(
                    out=dst, in0=turns[:], scalar=-two_pi, in1=src, op0=ALU.mult, op1=ALU.add
                )

            return [
                tensor(phase[:], ts_wide, w_wide, ALU.mult),
                tensor(phase[:], phase[:], b_wide, ALU.add),
                scalar(turns[:], phase[:], 1.0 / (2.0 * math.pi), ROUND_MAGIC, ALU.mult, ALU.add),
                scalar(turns[:], turns[:], 1.0, -ROUND_MAGIC, ALU.mult, ALU.add),
                take_off(red, phase[:], TWO_PI_HIGH),
                take_off(red, red, TWO_PI_LOW),
                scalar(red, red, -SIN_LIMIT, SIN_LIMIT, ALU.max, ALU.min),
            ]

        def time_features(j):
            nc.scalar.activation(out=t2v[:, j, :, 1:T2V], in_=reduced[:, j, :, :], func=ACT.Sin)
            nc.scalar.activation(
                out=t2v[:, j, :, 0:1],
                in_=ts_sb[:, j, :].unsqueeze(2),
                func=ACT.Identity,
                scale=w0_f32[:],
                bias=b0_f32[:],
            )

        gamma_beta = const.tile([P, PACK, 2 * all_passes], F32)
        w_codes = const.tile([P, all_passes, D_OUT], U32, align_bytes=64)
        w_scales = const.tile([P, all_passes, D_OUT], U8, align_bytes=64)
        w_grouped = const.tile([P, all_passes, D_OUT, PACK], BF16, align_bytes=64)

        def turn_gamma_beta():
            gb_rows_f32 = const.tile([P, PACK, P], F32)
            nc.gpsimd.tensor_scalar(
                out=gb_rows_f32[:],
                in0=gb_rows[:].rearrange("c (p t) -> c t p", t=PACK),
                scalar1=1.0,
                scalar2=0.0,
                op0=ALU.mult,
                op1=ALU.add,
            )
            gb_turned = turned_pool.tile([P, PACK, P], F32, tag="turned")
            for t in range(PACK):
                nc.tensor.transpose(gb_turned[:, t, :], gb_rows_f32[:, t, :], identity[:])
            nc.scalar.copy(out=gamma_beta[:], in_=gb_turned[:, :, 0 : 2 * all_passes])

        def interleave_w(c):
            nc.scalar.copy(out=w_grouped[:, c, :, :], in_=w_raw[:, c, :, :].rearrange("p t n -> p n t"))

        def quantise_w(c):
            nc.vector.quantize_mx(
                out=w_codes[:, c, :].bitcast(FP8X4),
                scales=w_scales[:, c, :],
                in_=w_grouped[:, c, :, :].rearrange("p n t -> p (n t)"),
            )

        scalar_tile = GROUP - 1
        stats = {}
        mean_var = {}
        row_scale = {}
        row_shift = {}
        normalised = {}
        banks = {}
        planes = {}
        grouped = {}
        zn_codes = {}
        zn_scales = {}
        sums = {}

        def by_scalar(j, g, i):
            return (j, g) in groups[:2] and i == scalar_tile

        def new_stats(j, g):
            n = 2 * (kinds[j]["chunks"] + 1) * TRIPLE
            st = const.tile([P, GROUP, n + TRIPLE], F32, name="stats_%d_%d" % (j, g))
            nc.vector.memset(st[:, :, n : n + 2], 0.0)
            nc.vector.memset(st[:, :, n + 2 : n + TRIPLE], LN_EPS * kinds[j]["passes"] * K_PASS)
            if by_scalar(j, g, scalar_tile):
                nc.vector.memset(st[:, scalar_tile, TRIPLE : TRIPLE + 1], float(kinds[j]["d"]))
            stats[(j, g)] = st

        def row_statistics(j, g, i):
            chunks = kinds[j]["chunks"]
            width = kinds[j]["d"] // chunks
            for h in range(chunks):
                nc.vector.bn_stats(
                    out=stats[(j, g)][:, i, 2 * h * TRIPLE : 2 * (h + 1) * TRIPLE],
                    in_=x_sb[(j, g)][:, i, h * width : (h + 1) * width],
                )

        def scalar_statistics(j, g):
            i, d = scalar_tile, kinds[j]["d"]
            junk = small.tile([P, d], BF16, tag="junk", name="junk")
            neg_mean = small.tile([P, 1], F32, tag="neg_mean", name="neg_mean")
            row, triple = x_sb[(j, g)][:, i, :], stats[(j, g)][:, i, TRIPLE : 2 * TRIPLE]
            nc.scalar.activation(out=junk[:], in_=row, func=ACT.Copy, scale=-1.0 / d, accum_out=neg_mean[:])
            nc.scalar.activation(
                out=junk[:], in_=row, func=ACT.Square, bias=neg_mean[:], accum_out=triple[:, 2:3]
            )
            nc.scalar.mul(triple[:, 1:2], neg_mean[:], -1.0)

        def time_statistics(j, g, i):
            n = 2 * kinds[j]["chunks"]
            nc.vector.bn_stats(
                out=stats[(j, g)][:, i, n * TRIPLE : (n + 2) * TRIPLE], in_=t2v[:, j, g * GROUP + i, :]
            )

        def aggregate(j, g):
            mean_var[(j, g)] = small.tile([P, GROUP, 2], F32, tag="mean_var", name="mean_var")
            for i in range(GROUP):
                start = TRIPLE if by_scalar(j, g, i) else 0
                nc.vector.bn_aggr(out=mean_var[(j, g)][:, i, :], in_=stats[(j, g)][:, i, start:])

        def invert(j, g):
            scale = small.tile([P, GROUP], F32, tag="scale")
            nc.gpsimd.tensor_tensor(out=scale[:], in0=mean_var[(j, g)][:, :, 1], in1=neg_half[:], op=ALU.pow)
            row_scale[(j, g)] = scale

        def shift_rows(j, g):
            shift = small.tile([P, GROUP], F32, tag="shift")
            nc.vector.scalar_tensor_tensor(
                out=shift[:], in0=mean_var[(j, g)][:, :, 0], scalar=-1.0, in1=row_scale[(j, g)][:], op0=ALU.mult, op1=ALU.mult
            )
            row_shift[(j, g)] = shift

        def normalise(u, vector_tiles):
            j, g, c = units[u]
            scale, shift = row_scale[(j, g)], row_shift[(j, g)]
            xn = xn_pool.tile([P, GROUP, PACK, P], F32, tag="xn", name="xn")
            is_last = c == kinds[j]["passes"] - 1
            width = P - T2V_P if is_last else P
            for i in range(GROUP):
                dst = xn[:, i, :, 0:width]
                src = x_sb[(j, g)][:, i, c * K_PASS : c * K_PASS + width * PACK].rearrange("r (p t) -> r t p", t=PACK)
                if i < GROUP - vector_tiles:
                    nc.scalar.activation(
                        out=dst, in_=src, func=ACT.Identity, scale=scale[:, i : i + 1], bias=shift[:, i : i + 1]
                    )
                else:
                    nc.vector.tensor_scalar(
                        out=dst,
                        in0=src,
                        scalar1=mean_var[(j, g)][:, i, 0:1],
                        scalar2=scale[:, i : i + 1],
                        op0=ALU.subtract,
                        op1=ALU.mult,
                    )
            if is_last:
                for i in range(GROUP):
                    nc.scalar.activation(
                        out=xn[:, i, :, width:P],
                        in_=t2v[:, j, g * GROUP + i, :].rearrange("r (p t) -> r t p", t=PACK),
                        func=ACT.Identity,
                        scale=scale[:, i : i + 1],
                        bias=shift[:, i : i + 1],
                    )
            normalised[u] = xn

        def turn(u):
            for t in range(PACK):
                bank = turned_pool.tile([P, GROUP_COLS], F32, tag="turned", name="turned")
                for i in range(GROUP):
                    nc.tensor.transpose(bank[:, i * P : (i + 1) * P], normalised[u][:, i, t, :], identity[:])
                banks[(u, t)] = bank

        def leave(u):
            j, g, c = units[u]
            planes[u] = work.tile([P, PACK, GROUP_COLS], BF16, tag="planes", name="planes")
            col = kinds[j]["first"] + c
            for t in range(PACK):
                nc.scalar.activation(
                    out=planes[u][:, t, :],
                    in_=banks[(u, t)][:],
                    func=ACT.Identity,
                    scale=gamma_beta[:, t, col : col + 1],
                    bias=gamma_beta[:, t, all_passes + col : all_passes + col + 1],
                )

        def interleave(u, cols):
            if u not in grouped:
                grouped[u] = work.tile([P, GROUP_COLS, PACK], BF16, tag="grouped", align_bytes=64, name="grouped")
            nc.vector.tensor_copy(
                out=grouped[u][:, cols, :].rearrange("p (n r) t -> p n t r", r=4),
                in_=planes[u][:, :, cols].rearrange("p t (n r) -> p n t r", r=4),
            )

        def quantise(u, cols):
            if u not in zn_codes:
                zn_codes[u] = work.tile([P, GROUP_COLS], U32, tag="codes", align_bytes=64, name="codes")
                zn_scales[u] = work.tile([P, GROUP_COLS], U8, tag="scales", align_bytes=64, name="scales")
            nc.vector.quantize_mx(
                out=zn_codes[u][:, cols].bitcast(FP8X4),
                scales=zn_scales[u][:, cols],
                in_=grouped[u][:, cols, :].rearrange("p n t -> p (n t)"),
            )

        def multiply(u):
            j, g, c = units[u]
            passes = c + 1
            for half in range(2):
                acc = acc_pool.tile([P, 2, D_OUT], F32, tag="acc", name="acc")
                for s in range(2):
                    i = half * 2 + s
                    for k in range(passes):
                        unit = u - c + k
                        nc.tensor.matmul_mx(
                            out=acc[:, s, :],
                            lhsT=zn_codes[unit][:, i * P : (i + 1) * P].bitcast(FP8X4),
                            lhsT_scale=zn_scales[unit][:, i * P : (i + 1) * P],
                            rhs=w_codes[:, kinds[j]["first"] + k, :].bitcast(FP8X4),
                            rhs_scale=w_scales[:, kinds[j]["first"] + k, :],
                            start=(k == 0),
                            stop=(k == passes - 1),
                        )
                sums[(u, half)] = acc

        def gelu_and_store(u, halves):
            j, g, c = units[u]
            out_rows = out[j].rearrange("(p i) n -> p i n", i=ROW_TILES)
            result = work.tile([P, GROUP, D_OUT], F32, tag="result", name="result")
            for half in halves:
                tiles = slice(half * 2, half * 2 + 2)
                nc.scalar.activation(out=result[:, tiles, :], in_=sums[(u, half)][:], func=ACT.Gelu)
            tiles = slice(halves[0] * 2, halves[-1] * 2 + 2)
            first_row = g * GROUP
            nc.sync.dma_start(
                out=out_rows[:, first_row + tiles.start : first_row + tiles.stop, :], in_=result[:, tiles, :]
            )

        pieces = []
        for j, g in groups:
            n = kinds[j]["passes"]
            for c in range(n):
                pieces.append((j, g, range(c * GROUP // n, (c + 1) * GROUP // n), c == n - 1))

        n_units = len(units)

        def is_last_pass(u):
            j, g, c = units[u]
            return c == kinds[j]["passes"] - 1

        def x_steps(k):
            j, g, tiles, ends_group = pieces[k]
            return [lambda i=i: row_statistics(j, g, i) for i in tiles if not by_scalar(j, g, i)]

        def time_steps(k):
            j, g, tiles, ends_group = pieces[k]
            return [lambda i=i: time_statistics(j, g, i) for i in tiles]

        def run(steps):
            for step in steps:
                step()

        def weave(*chains):
            for k in range(max(len(chain) for chain in chains)):
                for chain in chains:
                    if k < len(chain):
                        chain[k]()

        def vector_tiles(u):
            if u < 2:
                return 0
            return 1 if u + LOOKAHEAD <= n_units else GROUP

        def column_parts(u):
            half = GROUP_COLS // 2
            return [slice(0, half), slice(half, GROUP_COLS)] if u == n_units - 1 else [slice(0, GROUP_COLS)]

        with tc.manual_schedule():
            nc.scalar.activation(out=warm[:], in_=zero[:], func=ACT.Sin)
            nc.scalar.copy(out=b0_f32[:], in_=b_sb[:, 0:1])
            for group in groups:
                new_stats(*group)
            bill_phase, version_phase = phase_steps(BILL), phase_steps(VERSION)
            second_x = x_steps(1)
            weave(bill_phase[:3], version_phase[:3])
            weave(bill_phase[3:], x_steps(0))
            scalar_statistics(*groups[0])
            nc.scalar.copy(out=w0_f32[:], in_=w0_sb[:])
            interleave_w(0)
            time_features(BILL)
            turn_gamma_beta()
            weave(version_phase[3:5], second_x[:1])
            run(time_steps(0))
            scalar_statistics(*groups[1])
            aggregate(*groups[0])
            invert(*groups[0])
            interleave_w(1)
            weave(version_phase[5:], second_x[1:])
            shift_rows(*groups[0])
            normalise(0, vector_tiles(0))
            turn(0)
            run(time_steps(1))
            third_x = x_steps(2)
            run(third_x[:1])
            aggregate(*groups[1])
            invert(*groups[1])
            time_features(VERSION)
            nc.scalar.activation(out=warm[:], in_=zero[:], func=ACT.Gelu)
            run(third_x[1:])
            shift_rows(*groups[1])
            normalise(1, vector_tiles(1))
            run(time_steps(2))
            run(x_steps(3))
            run(time_steps(3))
            for s in range(n_units + 2):
                k = s + LOOKAHEAD
                closes = k - 1 < n_units and pieces[k - 1][3]
                multiplies = 0 <= s - 1 < n_units and is_last_pass(s - 1)
                if closes:
                    aggregate(*pieces[k - 1][:2])
                    invert(*pieces[k - 1][:2])
                if s < n_units:
                    leave(s)
                if 0 <= s - 1 < n_units:
                    for cols in column_parts(s - 1):
                        interleave(s - 1, cols)
                if k < n_units:
                    run(x_steps(k))
                    run(time_steps(k))
                if closes:
                    shift_rows(*pieces[k - 1][:2])
                if s == 0:
                    interleave_w(2)
                    quantise_w(0)
                if s == 2:
                    quantise_w(1)
                    quantise_w(2)
                if multiplies:
                    for u in range(s - 1 - units[s - 1][2], s):
                        for cols in column_parts(u):
                            quantise(u, cols)
                if s + 2 < n_units:
                    normalise(s + 2, vector_tiles(s + 2))
                if 0 <= s - 2 and is_last_pass(s - 2):
                    for halves in [[0], [1]] if s - 2 == n_units - 1 else [[0, 1]]:
                        gelu_and_store(s - 2, halves)
                if s + 1 < n_units:
                    turn(s + 1)
                if multiplies:
                    multiply(s - 1)
